import numpy as np
import ml_dtypes


def mxq(x, axis, fmt="e4m3"):
    dtype, down = {"e4m3": (ml_dtypes.float8_e4m3fn, 7), "e5m2": (ml_dtypes.float8_e5m2, 14)}[fmt]
    v = np.moveaxis(np.asarray(x, np.float32).astype(ml_dtypes.bfloat16).astype(np.float64), axis, -1)
    blocks = v.reshape(v.shape[:-1] + (-1, 32))
    amax = np.abs(blocks).max(-1, keepdims=True)
    byte = np.maximum(np.where(amax > 0, np.frexp(amax)[1] - 1 + 127, 0) - down, 1)
    scale = np.exp2(byte - 127.0)
    codes = (blocks / scale).astype(np.float32).astype(dtype).astype(np.float64)
    return np.moveaxis((codes * scale).reshape(v.shape), -1, axis)


WIDE = False


def mx_kscale(k):
    if not WIDE:
        return np.ones(k)
    levels = np.array([10, -10, 5, -5, 0])
    a = np.random.permutation(np.resize(levels, k // 512 * 4)).reshape(k // 512, 4)
    idx = np.arange(k)
    return np.exp2(a[idx // 512, idx % 128 // 32])


BF16 = ml_dtypes.bfloat16


def bf(x):
    return np.asarray(x, np.float32).astype(BF16)


def f64(x):
    return np.asarray(x).astype(np.float64)


E2M1 = np.array([0.0, 0.5, 1.0, 1.5, 2.0, 3.0, 4.0, 6.0, -0.0, -0.5, -1.0, -1.5, -2.0, -3.0, -4.0, -6.0])


def pack_weight(w, fmt):
    k, n = w.shape
    w = f64(bf(w)).reshape(k // 32, 32, n)
    amax = np.abs(w).max(1)
    if fmt == "e4m3":
        byte = np.frexp(amax)[1] - 1 + 127 - 7
    else:
        mant, ex = np.frexp(amax / 6.0)
        byte = np.where(mant > 0.5, ex, ex - 1) + 127
    byte = np.clip(np.where(amax > 0, byte, 1), 1, 254)
    scaled = (w * np.exp2(127.0 - byte)[:, None, :]).reshape(k, n).astype(np.float32)
    by_word = np.ascontiguousarray(scaled.reshape(k // 512, 128, 4, n).transpose(0, 1, 3, 2))
    if fmt == "e4m3":
        words = by_word.astype(ml_dtypes.float8_e4m3fn).view(np.uint8)
    else:
        c = by_word.astype(ml_dtypes.float4_e2m1fn).view(np.uint8) & 0xF
        words = c[..., 0::2] | (c[..., 1::2] << 4)
    return np.ascontiguousarray(words), np.ascontiguousarray(byte.astype(np.uint8).reshape(k // 512, 16, n))


def unpack_weight(words, scales, fmt):
    g, p, n, _ = words.shape
    if fmt == "e4m3":
        vals = np.ascontiguousarray(words).view(ml_dtypes.float8_e4m3fn).astype(np.float64)
    else:
        nib = np.empty((g, p, n, 4), np.uint8)
        nib[..., 0::2] = words & 0xF
        nib[..., 1::2] = words >> 4
        vals = E2M1[nib]
    vals = vals * np.repeat(np.exp2(scales.astype(np.float64) - 127.0), 8, axis=1)[..., None]
    return vals.transpose(0, 1, 3, 2).reshape(g * 512, n)


B, D, R = 2048, 2048, 128
FMT = "e4m3"


def softplus(v):
    return np.log1p(np.exp(v))


def setup_inputs():
    s = mx_kscale(D)
    w = 1.0 / np.sqrt(D)
    x = bf(np.random.standard_normal((B, D)) * s)
    state_re = bf(np.random.standard_normal((B, R)))
    state_im = bf(np.random.standard_normal((B, R)))
    W_dt_words, W_dt_scales = pack_weight((np.random.standard_normal((R, D)) * 0.5 * w / s).T, FMT)
    b_dt = bf(np.random.standard_normal(R) * 0.3)
    W_ph_words, W_ph_scales = pack_weight((np.random.standard_normal((R, D)) * 0.5 * w / s).T, FMT)
    b_ph = bf(np.random.standard_normal(R) * 0.3)
    W_B_words, W_B_scales = pack_weight((np.random.standard_normal((R, D)) * w / s).T, FMT)
    A_real = bf(np.random.standard_normal(R) * 0.5)
    A_imag = bf(np.random.standard_normal(R) * 0.5)
    return {"x": x,
            "state_re": state_re,
            "state_im": state_im,
            "W_dt_words": W_dt_words,
            "W_dt_scales": W_dt_scales,
            "b_dt": b_dt,
            "W_ph_words": W_ph_words,
            "W_ph_scales": W_ph_scales,
            "b_ph": b_ph,
            "W_B_words": W_B_words,
            "W_B_scales": W_B_scales,
            "A_real": A_real,
            "A_imag": A_imag}


def reference(x, state_re, state_im, W_dt_words, W_dt_scales, b_dt, W_ph_words, W_ph_scales, b_ph, W_B_words, W_B_scales, A_real, A_imag):
    xq = mxq(f64(x), 1, "e4m3")
    dt = softplus((xq @ unpack_weight(W_dt_words, W_dt_scales, FMT)) + f64(b_dt))
    phase = np.tanh((xq @ unpack_weight(W_ph_words, W_ph_scales, FMT)) + f64(b_ph)) * np.pi
    decay = np.exp(-dt * np.exp(f64(A_real)))
    angle = dt * f64(A_imag) + phase
    B_val = xq @ unpack_weight(W_B_words, W_B_scales, FMT)
    cos = np.cos(angle)
    sin = np.sin(angle)
    new_re = (f64(state_re) * cos - f64(state_im) * sin) * decay + B_val
    new_im = (f64(state_re) * sin + f64(state_im) * cos) * decay
    return new_re, new_im

@@ -1,0 +1,315 @@
+import math
+from contextlib import ExitStack
+
+import concourse.masks as masks
+import concourse.mybir as mybir
+
+F32 = mybir.dt.float32
+BF16 = mybir.dt.bfloat16
+I32 = mybir.dt.int32
+U32 = mybir.dt.uint32
+U8 = mybir.dt.uint8
+FP8X4 = mybir.dt.float8_e4m3fn_x4
+ALU = mybir.AluOpType
+FUNC = mybir.ActivationFunctionType
+
+P = 128
+ROWS = 2048
+K = 2048
+CH = 128
+K_PASS = 512
+GROUPS = K // K_PASS
+WORDS = K_PASS // 2
+ROW_TILES = ROWS // P
+PAIR = 2
+PAIR_ROWS = PAIR * P
+PAIRS = ROW_TILES // PAIR
+HALVES = 2
+HALF_PAIRS = PAIRS // HALVES
+CHUNK = 512
+HALF_CHUNKS = ROWS // HALVES // CHUNK
+DT = 0
+PH = 1
+BV = 2
+
+EXP_CAP = math.exp(30.0)
+ROUND = 1.5 * 2.0**23
+
+FLOPS = 2 * ROWS * K * 3 * CH
+
+
+def tile_mamba3mimoblock_pa_kernel(
+    tc,
+    x,
+    state_re,
+    state_im,
+    W_dt_words,
+    W_dt_scales,
+    b_dt,
+    W_ph_words,
+    W_ph_scales,
+    b_ph,
+    W_B_words,
+    W_B_scales,
+    A_real,
+    A_imag,
+    out_0,
+    out_1,
+):
+    nc = tc.nc
+    x_rows = x.rearrange("(p t) k -> p t k", t=ROW_TILES)
+    out_rows = [o.rearrange("(p t) c -> p t c", t=ROW_TILES) for o in (out_0, out_1)]
+
+    with ExitStack() as stack:
+        keep = stack.enter_context(tc.tile_pool(name="keep", bufs=1))
+        stage = stack.enter_context(tc.tile_pool(name="stage", bufs=2))
+        banks = stack.enter_context(tc.psum_pool(name="banks", bufs=6))
+        sums = stack.enter_context(tc.psum_pool(name="sums", bufs=2))
+        stack.enter_context(tc.manual_schedule())
+
+        x_sb = keep.tile([P, ROW_TILES, K], BF16)
+        codes = keep.tile([P, PAIRS, GROUPS, PAIR_ROWS], U32, align_bytes=64)
+        x_scales = keep.tile([P, PAIRS, GROUPS, PAIR_ROWS], U8, align_bytes=64)
+        w_codes = keep.tile([P, 3, GROUPS, CH], U32, align_bytes=64)
+        w_scales = keep.tile([P, 3, GROUPS, CH], U8, align_bytes=64)
+        state = keep.tile([P, 3, ROW_TILES, CH], BF16)
+        ident = keep.tile([P, P], F32)
+        soft = keep.tile([P, ROWS], F32)
+        lin = keep.tile([P, ROWS], F32)
+        turn = keep.tile([P, ROWS], F32)
+        frac = keep.tile([P, ROWS], F32)
+        cosd = keep.tile([P, ROWS], F32)
+        sind = keep.tile([P, ROWS], F32)
+        decay = keep.tile([P, ROWS], F32)
+
+        def load_x(i):
+            for h in range(2):
+                part = (slice(None), slice(PAIR * i, PAIR * (i + 1)), slice(K // 2 * h, K // 2 * (h + 1)))
+                nc.sync.dma_start(out=x_sb[part], in_=x_rows[part])
+
+        def load_weight_codes(w, words):
+            nc.sync.dma_start(
+                out=w_codes[:, w].bitcast(I32),
+                in_=words.rearrange("g p n t -> p g (n t)").bitcast(I32),
+            )
+
+        def load_weight_scales(queue, w, scales):
+            by_r = scales.rearrange("g (a r) n -> r a g n", r=4)
+            for r in range(4):
+                queue.dma_start(out=w_scales[r:P:32, w].bitcast(F32), in_=by_r[r].bitcast(F32))
+
+        nc.vector.memset(w_scales[:].rearrange("p w g n -> p (w g n)").bitcast(I32), 0)
+        masks.make_identity(nc, ident[:])
+
+        vec_rows = keep.tile([P, P], BF16)
+        nc.vector.memset(vec_rows[:], 0.0)
+        half_pi = keep.tile([P, 1], F32)
+        nc.vector.memset(half_pi[:], 0.5)
+        nc.vector.tensor_scalar_mul(out=half_pi[:], in0=half_pi[:], scalar1=math.pi)
+
+        load_weight_scales(nc.scalar, DT, W_dt_scales)
+        load_x(0)
+        load_weight_scales(nc.scalar, PH, W_ph_scales)
+        for j, vec in enumerate((b_dt, b_ph, A_real, A_imag)):
+            nc.gpsimd.dma_start(
+                out=vec_rows[j : j + 1, :].bitcast(F32),
+                in_=vec.rearrange("(o n) -> o n", o=1).bitcast(F32),
+            )
+        load_weight_scales(nc.gpsimd, BV, W_B_scales)
+        load_x(1)
+        load_weight_codes(DT, W_dt_words)
+        load_weight_codes(PH, W_ph_words)
+        load_x(2)
+        load_x(3)
+        load_weight_codes(BV, W_B_words)
+        nc.sync.dma_start(out=state[:, 1], in_=state_re.rearrange("(p t) c -> p t c", t=ROW_TILES))
+        nc.sync.dma_start(out=state[:, 2], in_=state_im.rearrange("(p t) c -> p t c", t=ROW_TILES))
+        for i in range(4, PAIRS):
+            load_x(i)
+
+        grouped_of = {}
+
+        def transpose_x(i):
+            grouped = stage.tile([P, GROUPS, 4 * PAIR_ROWS], BF16, align_bytes=64)
+            grouped_of[i] = grouped
+            for g in range(GROUPS):
+                flipped = banks.tile([P, 2, PAIR_ROWS], F32, tag="bank")
+                for j in range(PAIR):
+                    words = x_sb[:, PAIR * i + j, :].bitcast(F32)
+                    for u in range(2):
+                        nc.tensor.transpose(
+                            out=flipped[:, u, P * j : P * (j + 1)],
+                            in_=words[:, WORDS * g + u : WORDS * (g + 1) : 2],
+                            identity=ident[:],
+                        )
+                copy = nc.scalar.copy if g % 2 == 0 else nc.vector.tensor_copy
+                copy(
+                    out=grouped[:, g, :].bitcast(F32).rearrange("p (r u) -> p r u", u=2),
+                    in_=flipped[:].rearrange("p u r -> p r u"),
+                )
+
+        def quantise_x(i):
+            nc.vector.quantize_mx(
+                out=codes[:, i].rearrange("p g r -> p (g r)").bitcast(FP8X4),
+                scales=x_scales[:, i].rearrange("p g r -> p (g r)"),
+                in_=grouped_of[i][:].rearrange("p g c -> p (g c)"),
+            )
+
+        def project(i):
+            acc = sums.tile([P, 2, PAIR_ROWS], F32)
+            for w in (DT, PH):
+                for g in range(GROUPS):
+                    nc.tensor.matmul_mx(
+                        out=acc[:, w, :],
+                        lhsT=w_codes[:, w, g, :].bitcast(FP8X4),
+                        lhsT_scale=w_scales[:, w, g, :],
+                        rhs=codes[:, i, g, :].bitcast(FP8X4),
+                        rhs_scale=x_scales[:, i, g, :],
+                        start=(g == 0),
+                        stop=(g == GROUPS - 1),
+                    )
+            cols = slice(PAIR_ROWS * i, PAIR_ROWS * (i + 1))
+            nc.scalar.activation(out=soft[:, cols], in_=acc[:, DT, :], func=FUNC.Exp, bias=bias_dt[:])
+            nc.scalar.activation(out=lin[:, cols], in_=acc[:, DT, :], func=FUNC.Identity, bias=bias_dt[:])
+            nc.scalar.activation(out=turn[:, cols], in_=acc[:, PH, :], func=FUNC.Tanh, bias=bias_ph[:])
+            nc.gpsimd.tensor_scalar(
+                out=soft[:, cols], in0=soft[:, cols], scalar1=EXP_CAP, scalar2=1.0, op0=ALU.min, op1=ALU.add
+            )
+
+        def stream(i):
+            if i >= 1:
+                quantise_x(i - 1)
+            if i < PAIRS:
+                transpose_x(i)
+            if i >= 1:
+                project(i - 1)
+
+        def spread_vectors():
+            vec_f32 = keep.tile([P, P], F32)
+            nc.vector.tensor_copy(out=vec_f32[:], in_=vec_rows[:])
+            vec_cols = banks.tile([P, P], F32, tag="bank")
+            nc.tensor.transpose(out=vec_cols[:], in_=vec_f32[:], identity=ident[:])
+            nc.vector.tensor_copy(out=bias_dt[:], in_=vec_cols[:, 0:1])
+            nc.vector.tensor_copy(out=bias_ph[:], in_=vec_cols[:, 1:2])
+            nc.vector.tensor_copy(out=a_real[:], in_=vec_cols[:, 2:3])
+            nc.vector.tensor_scalar_mul(out=turns_per_dt[:], in0=vec_cols[:, 3:4], scalar1=1.0 / math.pi)
+            nc.scalar.activation(out=neg_rate[:], in_=a_real[:], func=FUNC.Exp)
+            nc.vector.tensor_scalar_mul(out=neg_rate[:], in0=neg_rate[:], scalar1=-1.0)
+
+        bias_dt = keep.tile([P, 1], F32)
+        bias_ph = keep.tile([P, 1], F32)
+        a_real = keep.tile([P, 1], F32)
+        turns_per_dt = keep.tile([P, 1], F32)
+        neg_rate = keep.tile([P, 1], F32)
+
+        def chunks(h):
+            return [slice(CHUNK * c, CHUNK * (c + 1)) for c in range(HALF_CHUNKS * h, HALF_CHUNKS * (h + 1))]
+
+        def logarithm(h):
+            for cols in chunks(h):
+                nc.scalar.activation(out=soft[:, cols], in_=soft[:, cols], func=FUNC.Ln)
+
+        def step_size(h):
+            for cols in chunks(h):
+                nc.vector.tensor_tensor(out=soft[:, cols], in0=soft[:, cols], in1=lin[:, cols], op=ALU.max)
+
+        def decay_factor(h):
+            for cols in chunks(h):
+                nc.scalar.activation(out=decay[:, cols], in_=soft[:, cols], func=FUNC.Exp, scale=neg_rate[:])
+
+        def angle(h):
+            for cols in chunks(h):
+                nc.vector.scalar_tensor_tensor(
+                    out=turn[:, cols], in0=soft[:, cols], scalar=turns_per_dt[:], in1=turn[:, cols],
+                    op0=ALU.mult, op1=ALU.add,
+                )
+            for cols in chunks(h):
+                nc.vector.tensor_scalar(
+                    out=frac[:, cols], in0=turn[:, cols], scalar1=0.5, scalar2=ROUND, op0=ALU.mult, op1=ALU.add
+                )
+            for cols in chunks(h):
+                nc.vector.tensor_scalar(
+                    out=frac[:, cols], in0=frac[:, cols], scalar1=ROUND, scalar2=2.0, op0=ALU.subtract, op1=ALU.mult
+                )
+            for cols in chunks(h):
+                nc.vector.tensor_tensor(out=frac[:, cols], in0=turn[:, cols], in1=frac[:, cols], op=ALU.subtract)
+
+        def sin_and_cos(h):
+            for cols in chunks(h):
+                nc.scalar.activation(out=cosd[:, cols], in_=frac[:, cols], func=FUNC.Abs)
+                nc.scalar.activation(out=sind[:, cols], in_=frac[:, cols], func=FUNC.Sin, scale=math.pi)
+                nc.scalar.activation(
+                    out=cosd[:, cols], in_=cosd[:, cols], func=FUNC.Sin, scale=-math.pi, bias=half_pi[:]
+                )
+
+        def scale_by_decay(cols):
+            nc.vector.tensor_tensor(out=sind[:, cols], in0=sind[:, cols], in1=decay[:, cols], op=ALU.mult)
+            nc.vector.tensor_tensor(out=cosd[:, cols], in0=cosd[:, cols], in1=decay[:, cols], op=ALU.mult)
+
+        def rotate(i):
+            tiles = slice(PAIR * i, PAIR * (i + 1))
+            cos_sin = banks.tile([P, 2, PAIR, CH], F32, tag="bank")
+            for s, source in enumerate((cosd, sind)):
+                for j in range(PAIR):
+                    first = PAIR_ROWS * i + P * j
+                    nc.tensor.transpose(out=cos_sin[:, s, j, :], in_=source[:, first : first + P], identity=ident[:])
+            b_val = banks.tile([P, PAIR, CH], F32, tag="bank")
+            for j in range(PAIR):
+                rows = slice(P * j, P * (j + 1))
+                for g in range(GROUPS):
+                    nc.tensor.matmul_mx(
+                        out=b_val[:, j, :],
+                        lhsT=codes[:, i, g, rows].bitcast(FP8X4),
+                        lhsT_scale=x_scales[:, i, g, rows],
+                        rhs=w_codes[:, BV, g, :].bitcast(FP8X4),
+                        rhs_scale=w_scales[:, BV, g, :],
+                        start=(g == 0),
+                        stop=(g == GROUPS - 1),
+                    )
+            both = [P, 2, PAIR, CH]
+            by_cos = stage.tile(both, F32)
+            by_sin = stage.tile(both, F32)
+            result = stage.tile(both, F32)
+            nc.vector.tensor_tensor(
+                out=by_cos[:], in0=state[:, 1:3, tiles, :], in1=cos_sin[:, 0:1].to_broadcast(both), op=ALU.mult
+            )
+            nc.vector.tensor_tensor(
+                out=by_sin[:], in0=state[:, 0:2, tiles, :], in1=cos_sin[:, 1:2].to_broadcast(both), op=ALU.mult
+            )
+            nc.vector.tensor_tensor(out=by_cos[:, 0], in0=by_cos[:, 0], in1=b_val[:], op=ALU.add)
+            nc.gpsimd.tensor_tensor(out=result[:], in0=by_cos[:], in1=by_sin[:], op=ALU.add)
+            for s in range(2):
+                nc.sync.dma_start(out=out_rows[s][:, tiles, :], in_=result[:, s])
+
+        transpose_x(0)
+        quantise_x(0)
+        transpose_x(1)
+        spread_vectors()
+        project(0)
+        for i in range(2, HALF_PAIRS + 1):
+            stream(i)
+        nc.vector.tensor_scalar_mul(out=state[:, 0], in0=state[:, 2], scalar1=-1.0)
+        logarithm(0)
+        stream(HALF_PAIRS + 1)
+        step_size(0)
+        decay_factor(0)
+        angle(0)
+        stream(HALF_PAIRS + 2)
+        sin_and_cos(0)
+        stream(HALF_PAIRS + 3)
+        for cols in chunks(0):
+            scale_by_decay(cols)
+        stream(HALF_PAIRS + 4)
+        logarithm(1)
+        rotate(0)
+        rotate(1)
+        step_size(1)
+        decay_factor(1)
+        angle(1)
+        sin_and_cos(1)
+        rotate(2)
+        rotate(3)
+        for c, cols in enumerate(chunks(1)):
+            scale_by_decay(cols)
+            rotate(HALF_PAIRS + 2 * c)
+            rotate(HALF_PAIRS + 2 * c + 1)

@@ -172,7 +172,7 @@ def tile_mamba3mimoblock_pa_kernel(
             nc.scalar.activation(out=soft[:, cols], in_=acc[:, DT, :], func=FUNC.Exp, bias=bias_dt[:])
             nc.scalar.activation(out=lin[:, cols], in_=acc[:, DT, :], func=FUNC.Identity, bias=bias_dt[:])
             nc.scalar.activation(out=turn[:, cols], in_=acc[:, PH, :], func=FUNC.Tanh, bias=bias_ph[:])
-            nc.gpsimd.tensor_scalar(
+            nc.vector.tensor_scalar(
                 out=soft[:, cols], in0=soft[:, cols], scalar1=EXP_CAP, scalar2=1.0, op0=ALU.min, op1=ALU.add
             )
 
@@ -277,7 +277,7 @@ def tile_mamba3mimoblock_pa_kernel(
                 out=by_sin[:], in0=state[:, 0:2, tiles, :], in1=cos_sin[:, 1:2].to_broadcast(both), op=ALU.mult
             )
             nc.vector.tensor_tensor(out=by_cos[:, 0], in0=by_cos[:, 0], in1=b_val[:], op=ALU.add)
-            nc.gpsimd.tensor_tensor(out=result[:], in0=by_cos[:], in1=by_sin[:], op=ALU.add)
+            nc.vector.tensor_tensor(out=result[:], in0=by_cos[:], in1=by_sin[:], op=ALU.add)
             for s in range(2):
                 nc.sync.dma_start(out=out_rows[s][:, tiles, :], in_=result[:, s])
 

@@ -93,10 +93,10 @@ def tile_mamba3mimoblock_pa_kernel(
                 in_=words.rearrange("g p n t -> p g (n t)").bitcast(I32),
             )
 
-        def load_weight_scales(queue, w, scales):
+        def load_weight_scales(queue, view, w, scales):
             by_r = scales.rearrange("g (a r) n -> r a g n", r=4)
             for r in range(4):
-                queue.dma_start(out=w_scales[r:P:32, w].bitcast(F32), in_=by_r[r].bitcast(F32))
+                queue.dma_start(out=w_scales[r:P:32, w].bitcast(view), in_=by_r[r].bitcast(view))
 
         nc.vector.memset(w_scales[:].rearrange("p w g n -> p (w g n)").bitcast(I32), 0)
         masks.make_identity(nc, ident[:])
@@ -105,27 +105,24 @@ def tile_mamba3mimoblock_pa_kernel(
         nc.vector.memset(vec_rows[:], 0.0)
         half_pi = keep.tile([P, 1], F32)
         nc.vector.memset(half_pi[:], 0.5)
-        nc.vector.tensor_scalar_mul(out=half_pi[:], in0=half_pi[:], scalar1=math.pi)
+        nc.scalar.mul(out=half_pi[:], in_=half_pi[:], mul=math.pi)
 
-        load_weight_scales(nc.scalar, DT, W_dt_scales)
+        load_weight_scales(nc.scalar, F32, DT, W_dt_scales)
         load_x(0)
-        load_weight_scales(nc.scalar, PH, W_ph_scales)
-        for j, vec in enumerate((b_dt, b_ph, A_real, A_imag)):
-            nc.gpsimd.dma_start(
-                out=vec_rows[j : j + 1, :].bitcast(F32),
-                in_=vec.rearrange("(o n) -> o n", o=1).bitcast(F32),
-            )
-        load_weight_scales(nc.gpsimd, BV, W_B_scales)
+        load_weight_scales(nc.scalar, F32, PH, W_ph_scales)
         load_x(1)
         load_weight_codes(DT, W_dt_words)
         load_weight_codes(PH, W_ph_words)
+        for j, vec in enumerate((b_dt, b_ph, A_real, A_imag)):
+            nc.sync.dma_start(out=vec_rows[j : j + 1, :], in_=vec.rearrange("(o n) -> o n", o=1))
         load_x(2)
         load_x(3)
-        load_weight_codes(BV, W_B_words)
         nc.sync.dma_start(out=state[:, 1], in_=state_re.rearrange("(p t) c -> p t c", t=ROW_TILES))
         nc.sync.dma_start(out=state[:, 2], in_=state_im.rearrange("(p t) c -> p t c", t=ROW_TILES))
         for i in range(4, PAIRS):
             load_x(i)
+        load_weight_codes(BV, W_B_words)
+        load_weight_scales(nc.sync, I32, BV, W_B_scales)
 
         grouped_of = {}
 
@@ -172,7 +169,7 @@ def tile_mamba3mimoblock_pa_kernel(
             nc.scalar.activation(out=soft[:, cols], in_=acc[:, DT, :], func=FUNC.Exp, bias=bias_dt[:])
             nc.scalar.activation(out=lin[:, cols], in_=acc[:, DT, :], func=FUNC.Identity, bias=bias_dt[:])
             nc.scalar.activation(out=turn[:, cols], in_=acc[:, PH, :], func=FUNC.Tanh, bias=bias_ph[:])
-            nc.vector.tensor_scalar(
+            nc.gpsimd.tensor_scalar(
                 out=soft[:, cols], in0=soft[:, cols], scalar1=EXP_CAP, scalar2=1.0, op0=ALU.min, op1=ALU.add
             )
 
@@ -277,7 +274,7 @@ def tile_mamba3mimoblock_pa_kernel(
                 out=by_sin[:], in0=state[:, 0:2, tiles, :], in1=cos_sin[:, 1:2].to_broadcast(both), op=ALU.mult
             )
             nc.vector.tensor_tensor(out=by_cos[:, 0], in0=by_cos[:, 0], in1=b_val[:], op=ALU.add)
-            nc.vector.tensor_tensor(out=result[:], in0=by_cos[:], in1=by_sin[:], op=ALU.add)
+            nc.gpsimd.tensor_tensor(out=result[:], in0=by_cos[:], in1=by_sin[:], op=ALU.add)
             for s in range(2):
                 nc.sync.dma_start(out=out_rows[s][:, tiles, :], in_=result[:, s])
 
@@ -288,7 +285,7 @@ def tile_mamba3mimoblock_pa_kernel(
         project(0)
         for i in range(2, HALF_PAIRS + 1):
             stream(i)
-        nc.vector.tensor_scalar_mul(out=state[:, 0], in0=state[:, 2], scalar1=-1.0)
+        nc.gpsimd.tensor_scalar(out=state[:, 0], in0=state[:, 2], scalar1=-1.0, scalar2=0.0, op0=ALU.mult, op1=ALU.add)
         logarithm(0)
         stream(HALF_PAIRS + 1)
         step_size(0)
@@ -307,9 +304,12 @@ def tile_mamba3mimoblock_pa_kernel(
         decay_factor(1)
         angle(1)
         sin_and_cos(1)
+        first_chunk, second_chunk = chunks(1)
         rotate(2)
+        scale_by_decay(first_chunk)
         rotate(3)
-        for c, cols in enumerate(chunks(1)):
-            scale_by_decay(cols)
-            rotate(HALF_PAIRS + 2 * c)
-            rotate(HALF_PAIRS + 2 * c + 1)
+        rotate(4)
+        scale_by_decay(second_chunk)
+        rotate(5)
+        rotate(6)
+        rotate(7)

@@ -24,10 +24,8 @@ ROW_TILES = ROWS // P
 PAIR = 2
 PAIR_ROWS = PAIR * P
 PAIRS = ROW_TILES // PAIR
-HALVES = 2
-HALF_PAIRS = PAIRS // HALVES
-CHUNK = 512
-HALF_CHUNKS = ROWS // HALVES // CHUNK
+FIRST_BATCH = 5
+CHUNK_PAIRS = 2
 DT = 0
 PH = 1
 BV = 2
@@ -63,9 +61,12 @@ def tile_mamba3mimoblock_pa_kernel(
     with ExitStack() as stack:
         keep = stack.enter_context(tc.tile_pool(name="keep", bufs=1))
         stage = stack.enter_context(tc.tile_pool(name="stage", bufs=2))
+        turned = stack.enter_context(tc.tile_pool(name="turned", bufs=3))
         banks = stack.enter_context(tc.psum_pool(name="banks", bufs=6))
         sums = stack.enter_context(tc.psum_pool(name="sums", bufs=2))
-        stack.enter_context(tc.manual_schedule())
+        stack.enter_context(
+            tc.manual_schedule(engines={mybir.EngineType.PE, mybir.EngineType.Activation, mybir.EngineType.SP})
+        )
 
         x_sb = keep.tile([P, ROW_TILES, K], BF16)
         codes = keep.tile([P, PAIRS, GROUPS, PAIR_ROWS], U32, align_bytes=64)
@@ -169,7 +170,8 @@ def tile_mamba3mimoblock_pa_kernel(
             nc.scalar.activation(out=soft[:, cols], in_=acc[:, DT, :], func=FUNC.Exp, bias=bias_dt[:])
             nc.scalar.activation(out=lin[:, cols], in_=acc[:, DT, :], func=FUNC.Identity, bias=bias_dt[:])
             nc.scalar.activation(out=turn[:, cols], in_=acc[:, PH, :], func=FUNC.Tanh, bias=bias_ph[:])
-            nc.gpsimd.tensor_scalar(
+            capper = nc.gpsimd if i <= FIRST_BATCH else nc.vector
+            capper.tensor_scalar(
                 out=soft[:, cols], in0=soft[:, cols], scalar1=EXP_CAP, scalar2=1.0, op0=ALU.min, op1=ALU.add
             )
 
@@ -200,7 +202,10 @@ def tile_mamba3mimoblock_pa_kernel(
         neg_rate = keep.tile([P, 1], F32)
 
         def chunks(h):
-            return [slice(CHUNK * c, CHUNK * (c + 1)) for c in range(HALF_CHUNKS * h, HALF_CHUNKS * (h + 1))]
+            first, last = ((0, FIRST_BATCH), (FIRST_BATCH, PAIRS))[h]
+            return [
+                slice(PAIR_ROWS * c, PAIR_ROWS * min(c + CHUNK_PAIRS, last)) for c in range(first, last, CHUNK_PAIRS)
+            ]
 
         def logarithm(h):
             for cols in chunks(h):
@@ -264,9 +269,9 @@ def tile_mamba3mimoblock_pa_kernel(
                         stop=(g == GROUPS - 1),
                     )
             both = [P, 2, PAIR, CH]
-            by_cos = stage.tile(both, F32)
-            by_sin = stage.tile(both, F32)
-            result = stage.tile(both, F32)
+            by_cos = turned.tile(both, F32)
+            by_sin = turned.tile(both, F32)
+            result = turned.tile(both, F32)
             nc.vector.tensor_tensor(
                 out=by_cos[:], in0=state[:, 1:3, tiles, :], in1=cos_sin[:, 0:1].to_broadcast(both), op=ALU.mult
             )
@@ -274,7 +279,8 @@ def tile_mamba3mimoblock_pa_kernel(
                 out=by_sin[:], in0=state[:, 0:2, tiles, :], in1=cos_sin[:, 1:2].to_broadcast(both), op=ALU.mult
             )
             nc.vector.tensor_tensor(out=by_cos[:, 0], in0=by_cos[:, 0], in1=b_val[:], op=ALU.add)
-            nc.gpsimd.tensor_tensor(out=result[:], in0=by_cos[:], in1=by_sin[:], op=ALU.add)
+            adder = nc.vector if i == PAIRS - 1 else nc.gpsimd
+            adder.tensor_tensor(out=result[:], in0=by_cos[:], in1=by_sin[:], op=ALU.add)
             for s in range(2):
                 nc.sync.dma_start(out=out_rows[s][:, tiles, :], in_=result[:, s])
 
@@ -283,33 +289,32 @@ def tile_mamba3mimoblock_pa_kernel(
         transpose_x(1)
         spread_vectors()
         project(0)
-        for i in range(2, HALF_PAIRS + 1):
+        for i in range(2, FIRST_BATCH + 1):
             stream(i)
-        nc.gpsimd.tensor_scalar(out=state[:, 0], in0=state[:, 2], scalar1=-1.0, scalar2=0.0, op0=ALU.mult, op1=ALU.add)
+        nc.vector.tensor_scalar_mul(out=state[:, 0], in0=state[:, 2], scalar1=-1.0)
         logarithm(0)
-        stream(HALF_PAIRS + 1)
+        quantise_x(FIRST_BATCH)
+        transpose_x(FIRST_BATCH + 1)
         step_size(0)
         decay_factor(0)
         angle(0)
-        stream(HALF_PAIRS + 2)
+        project(FIRST_BATCH)
+        quantise_x(FIRST_BATCH + 1)
+        transpose_x(FIRST_BATCH + 2)
         sin_and_cos(0)
-        stream(HALF_PAIRS + 3)
         for cols in chunks(0):
             scale_by_decay(cols)
-        stream(HALF_PAIRS + 4)
+        project(FIRST_BATCH + 1)
+        quantise_x(FIRST_BATCH + 2)
+        project(FIRST_BATCH + 2)
         logarithm(1)
-        rotate(0)
-        rotate(1)
         step_size(1)
         decay_factor(1)
         angle(1)
+        for i in range(FIRST_BATCH):
+            rotate(i)
         sin_and_cos(1)
-        first_chunk, second_chunk = chunks(1)
-        rotate(2)
-        scale_by_decay(first_chunk)
-        rotate(3)
-        rotate(4)
-        scale_by_decay(second_chunk)
-        rotate(5)
-        rotate(6)
-        rotate(7)
+        for cols in chunks(1):
+            scale_by_decay(cols)
+        for i in range(FIRST_BATCH, PAIRS):
+            rotate(i)

@@ -248,6 +248,27 @@ def tile_mamba3mimoblock_pa_kernel(
             nc.vector.tensor_tensor(out=sind[:, cols], in0=sind[:, cols], in1=decay[:, cols], op=ALU.mult)
             nc.vector.tensor_tensor(out=cosd[:, cols], in0=cosd[:, cols], in1=decay[:, cols], op=ALU.mult)
 
+        b_val_of = {}
+
+        def b_products(h):
+            first, last = ((0, FIRST_BATCH), (FIRST_BATCH, PAIRS))[h]
+            for c in range(first, last, CHUNK_PAIRS):
+                b_bank = banks.tile([P, CHUNK_PAIRS, PAIR, CH], F32, tag="bank")
+                for i in range(c, min(c + CHUNK_PAIRS, last)):
+                    b_val_of[i] = b_bank[:, i - c]
+                    for j in range(PAIR):
+                        rows = slice(P * j, P * (j + 1))
+                        for g in range(GROUPS):
+                            nc.tensor.matmul_mx(
+                                out=b_bank[:, i - c, j, :],
+                                lhsT=codes[:, i, g, rows].bitcast(FP8X4),
+                                lhsT_scale=x_scales[:, i, g, rows],
+                                rhs=w_codes[:, BV, g, :].bitcast(FP8X4),
+                                rhs_scale=w_scales[:, BV, g, :],
+                                start=(g == 0),
+                                stop=(g == GROUPS - 1),
+                            )
+
         def rotate(i):
             tiles = slice(PAIR * i, PAIR * (i + 1))
             cos_sin = banks.tile([P, 2, PAIR, CH], F32, tag="bank")
@@ -255,19 +276,6 @@ def tile_mamba3mimoblock_pa_kernel(
                 for j in range(PAIR):
                     first = PAIR_ROWS * i + P * j
                     nc.tensor.transpose(out=cos_sin[:, s, j, :], in_=source[:, first : first + P], identity=ident[:])
-            b_val = banks.tile([P, PAIR, CH], F32, tag="bank")
-            for j in range(PAIR):
-                rows = slice(P * j, P * (j + 1))
-                for g in range(GROUPS):
-                    nc.tensor.matmul_mx(
-                        out=b_val[:, j, :],
-                        lhsT=codes[:, i, g, rows].bitcast(FP8X4),
-                        lhsT_scale=x_scales[:, i, g, rows],
-                        rhs=w_codes[:, BV, g, :].bitcast(FP8X4),
-                        rhs_scale=w_scales[:, BV, g, :],
-                        start=(g == 0),
-                        stop=(g == GROUPS - 1),
-                    )
             both = [P, 2, PAIR, CH]
             by_cos = turned.tile(both, F32)
             by_sin = turned.tile(both, F32)
@@ -278,7 +286,7 @@ def tile_mamba3mimoblock_pa_kernel(
             nc.vector.tensor_tensor(
                 out=by_sin[:], in0=state[:, 0:2, tiles, :], in1=cos_sin[:, 1:2].to_broadcast(both), op=ALU.mult
             )
-            nc.vector.tensor_tensor(out=by_cos[:, 0], in0=by_cos[:, 0], in1=b_val[:], op=ALU.add)
+            nc.vector.tensor_tensor(out=by_cos[:, 0], in0=by_cos[:, 0], in1=b_val_of[i], op=ALU.add)
             adder = nc.vector if i == PAIRS - 1 else nc.gpsimd
             adder.tensor_tensor(out=result[:], in0=by_cos[:], in1=by_sin[:], op=ALU.add)
             for s in range(2):
@@ -307,12 +315,14 @@ def tile_mamba3mimoblock_pa_kernel(
         project(FIRST_BATCH + 1)
         quantise_x(FIRST_BATCH + 2)
         project(FIRST_BATCH + 2)
+        b_products(0)
         logarithm(1)
         step_size(1)
         decay_factor(1)
         angle(1)
         for i in range(FIRST_BATCH):
             rotate(i)
+        b_products(1)
         sin_and_cos(1)
         for cols in chunks(1):
             scale_by_decay(cols)

@@ -31,7 +31,6 @@ PH = 1
 BV = 2
 
 EXP_CAP = math.exp(30.0)
-ROUND = 1.5 * 2.0**23
 
 FLOPS = 2 * ROWS * K * 3 * CH
 
@@ -78,6 +77,7 @@ def tile_mamba3mimoblock_pa_kernel(
         soft = keep.tile([P, ROWS], F32)
         lin = keep.tile([P, ROWS], F32)
         turn = keep.tile([P, ROWS], F32)
+        whole = keep.tile([P, ROWS], I32)
         frac = keep.tile([P, ROWS], F32)
         cosd = keep.tile([P, ROWS], F32)
         sind = keep.tile([P, ROWS], F32)
@@ -226,15 +226,11 @@ def tile_mamba3mimoblock_pa_kernel(
                     op0=ALU.mult, op1=ALU.add,
                 )
             for cols in chunks(h):
-                nc.vector.tensor_scalar(
-                    out=frac[:, cols], in0=turn[:, cols], scalar1=0.5, scalar2=ROUND, op0=ALU.mult, op1=ALU.add
-                )
+                nc.vector.tensor_scalar_mul(out=whole[:, cols], in0=turn[:, cols], scalar1=0.5)
             for cols in chunks(h):
-                nc.vector.tensor_scalar(
-                    out=frac[:, cols], in0=frac[:, cols], scalar1=ROUND, scalar2=2.0, op0=ALU.subtract, op1=ALU.mult
+                nc.vector.scalar_tensor_tensor(
+                    out=frac[:, cols], in0=whole[:, cols], scalar=-2.0, in1=turn[:, cols], op0=ALU.mult, op1=ALU.add
                 )
-            for cols in chunks(h):
-                nc.vector.tensor_tensor(out=frac[:, cols], in0=turn[:, cols], in1=frac[:, cols], op=ALU.subtract)
 
         def sin_and_cos(h):
             for cols in chunks(h):

@@ -106,6 +106,8 @@ def tile_mamba3mimoblock_pa_kernel(
         nc.vector.memset(vec_rows[:], 0.0)
         half_pi = keep.tile([P, 1], F32)
         nc.vector.memset(half_pi[:], 0.5)
+        warm = keep.tile([P, 1], F32)
+        nc.vector.memset(warm[:], 0.0)
         nc.scalar.mul(out=half_pi[:], in_=half_pi[:], mul=math.pi)
 
         load_weight_scales(nc.scalar, F32, DT, W_dt_scales)
@@ -240,8 +242,8 @@ def tile_mamba3mimoblock_pa_kernel(
                     out=cosd[:, cols], in_=cosd[:, cols], func=FUNC.Sin, scale=-math.pi, bias=half_pi[:]
                 )
 
-        def scale_by_decay(cols):
-            nc.vector.tensor_tensor(out=sind[:, cols], in0=sind[:, cols], in1=decay[:, cols], op=ALU.mult)
+        def scale_by_decay(cols, sine_engine):
+            sine_engine.tensor_tensor(out=sind[:, cols], in0=sind[:, cols], in1=decay[:, cols], op=ALU.mult)
             nc.vector.tensor_tensor(out=cosd[:, cols], in0=cosd[:, cols], in1=decay[:, cols], op=ALU.mult)
 
         b_val_of = {}
@@ -307,7 +309,7 @@ def tile_mamba3mimoblock_pa_kernel(
         transpose_x(FIRST_BATCH + 2)
         sin_and_cos(0)
         for cols in chunks(0):
-            scale_by_decay(cols)
+            scale_by_decay(cols, nc.gpsimd)
         project(FIRST_BATCH + 1)
         quantise_x(FIRST_BATCH + 2)
         project(FIRST_BATCH + 2)
@@ -315,12 +317,13 @@ def tile_mamba3mimoblock_pa_kernel(
         logarithm(1)
         step_size(1)
         decay_factor(1)
+        nc.scalar.activation(out=warm[:], in_=warm[:], func=FUNC.Sin)
         angle(1)
         for i in range(FIRST_BATCH):
             rotate(i)
         b_products(1)
         sin_and_cos(1)
         for cols in chunks(1):
-            scale_by_decay(cols)
+            scale_by_decay(cols, nc.vector)
         for i in range(FIRST_BATCH, PAIRS):
             rotate(i)

@@ -61,8 +61,8 @@ def tile_mamba3mimoblock_pa_kernel(
         keep = stack.enter_context(tc.tile_pool(name="keep", bufs=1))
         stage = stack.enter_context(tc.tile_pool(name="stage", bufs=2))
         turned = stack.enter_context(tc.tile_pool(name="turned", bufs=3))
-        banks = stack.enter_context(tc.psum_pool(name="banks", bufs=6))
-        sums = stack.enter_context(tc.psum_pool(name="sums", bufs=2))
+        banks = stack.enter_context(tc.psum_pool(name="banks", bufs=5))
+        sums = stack.enter_context(tc.psum_pool(name="sums", bufs=3))
         stack.enter_context(
             tc.manual_schedule(engines={mybir.EngineType.PE, mybir.EngineType.Activation, mybir.EngineType.SP})
         )
@@ -156,7 +156,14 @@ def tile_mamba3mimoblock_pa_kernel(
             )
 
         def project(i):
+            multiply(i)
+            first_functions(i)
+
+        acc_of = {}
+
+        def multiply(i):
             acc = sums.tile([P, 2, PAIR_ROWS], F32)
+            acc_of[i] = acc
             for w in (DT, PH):
                 for g in range(GROUPS):
                     nc.tensor.matmul_mx(
@@ -168,11 +175,15 @@ def tile_mamba3mimoblock_pa_kernel(
                         start=(g == 0),
                         stop=(g == GROUPS - 1),
                     )
+
+        def first_functions(i):
+            acc = acc_of[i]
             cols = slice(PAIR_ROWS * i, PAIR_ROWS * (i + 1))
             nc.scalar.activation(out=soft[:, cols], in_=acc[:, DT, :], func=FUNC.Exp, bias=bias_dt[:])
-            nc.scalar.activation(out=lin[:, cols], in_=acc[:, DT, :], func=FUNC.Identity, bias=bias_dt[:])
+            if i < FIRST_BATCH:
+                nc.scalar.activation(out=lin[:, cols], in_=acc[:, DT, :], func=FUNC.Identity, bias=bias_dt[:])
             nc.scalar.activation(out=turn[:, cols], in_=acc[:, PH, :], func=FUNC.Tanh, bias=bias_ph[:])
-            capper = nc.gpsimd if i <= FIRST_BATCH else nc.vector
+            capper = nc.gpsimd if i < FIRST_BATCH else nc.vector
             capper.tensor_scalar(
                 out=soft[:, cols], in0=soft[:, cols], scalar1=EXP_CAP, scalar2=1.0, op0=ALU.min, op1=ALU.add
             )
@@ -214,8 +225,16 @@ def tile_mamba3mimoblock_pa_kernel(
                 nc.scalar.activation(out=soft[:, cols], in_=soft[:, cols], func=FUNC.Ln)
 
         def step_size(h):
-            for cols in chunks(h):
-                nc.vector.tensor_tensor(out=soft[:, cols], in0=soft[:, cols], in1=lin[:, cols], op=ALU.max)
+            if h == 0:
+                for cols in chunks(h):
+                    nc.vector.tensor_tensor(out=soft[:, cols], in0=soft[:, cols], in1=lin[:, cols], op=ALU.max)
+            else:
+                for i in range(FIRST_BATCH, PAIRS):
+                    cols = slice(PAIR_ROWS * i, PAIR_ROWS * (i + 1))
+                    nc.vector.scalar_tensor_tensor(
+                        out=soft[:, cols], in0=acc_of[i][:, DT, :], scalar=bias_dt[:], in1=soft[:, cols],
+                        op0=ALU.add, op1=ALU.max,
+                    )
 
         def decay_factor(h):
             for cols in chunks(h):
@@ -236,15 +255,20 @@ def tile_mamba3mimoblock_pa_kernel(
 
         def sin_and_cos(h):
             for cols in chunks(h):
-                nc.scalar.activation(out=cosd[:, cols], in_=frac[:, cols], func=FUNC.Abs)
+                if h == 0:
+                    nc.scalar.activation(out=cosd[:, cols], in_=frac[:, cols], func=FUNC.Abs)
+                else:
+                    nc.vector.scalar_tensor_tensor(
+                        out=cosd[:, cols], in0=frac[:, cols], scalar=-1.0, in1=frac[:, cols], op0=ALU.mult, op1=ALU.max
+                    )
                 nc.scalar.activation(out=sind[:, cols], in_=frac[:, cols], func=FUNC.Sin, scale=math.pi)
                 nc.scalar.activation(
                     out=cosd[:, cols], in_=cosd[:, cols], func=FUNC.Sin, scale=-math.pi, bias=half_pi[:]
                 )
 
-        def scale_by_decay(cols, sine_engine):
-            sine_engine.tensor_tensor(out=sind[:, cols], in0=sind[:, cols], in1=decay[:, cols], op=ALU.mult)
-            nc.vector.tensor_tensor(out=cosd[:, cols], in0=cosd[:, cols], in1=decay[:, cols], op=ALU.mult)
+        def scale_by_decay(cols, engine):
+            engine.tensor_tensor(out=sind[:, cols], in0=sind[:, cols], in1=decay[:, cols], op=ALU.mult)
+            engine.tensor_tensor(out=cosd[:, cols], in0=cosd[:, cols], in1=decay[:, cols], op=ALU.mult)
 
         b_val_of = {}
 
@@ -297,23 +321,25 @@ def tile_mamba3mimoblock_pa_kernel(
         project(0)
         for i in range(2, FIRST_BATCH + 1):
             stream(i)
-        nc.vector.tensor_scalar_mul(out=state[:, 0], in0=state[:, 2], scalar1=-1.0)
+            if i == FIRST_BATCH - 1:
+                nc.vector.tensor_scalar_mul(out=state[:, 0], in0=state[:, 2], scalar1=-1.0)
         logarithm(0)
         quantise_x(FIRST_BATCH)
         transpose_x(FIRST_BATCH + 1)
         step_size(0)
         decay_factor(0)
         angle(0)
-        project(FIRST_BATCH)
+        multiply(FIRST_BATCH)
         quantise_x(FIRST_BATCH + 1)
         transpose_x(FIRST_BATCH + 2)
+        b_products(0)
         sin_and_cos(0)
         for cols in chunks(0):
             scale_by_decay(cols, nc.gpsimd)
+        first_functions(FIRST_BATCH)
         project(FIRST_BATCH + 1)
         quantise_x(FIRST_BATCH + 2)
         project(FIRST_BATCH + 2)
-        b_products(0)
         logarithm(1)
         step_size(1)
         decay_factor(1)

@@ -216,9 +216,10 @@ def tile_mamba3mimoblock_pa_kernel(
 
         def chunks(h):
             first, last = ((0, FIRST_BATCH), (FIRST_BATCH, PAIRS))[h]
-            return [
-                slice(PAIR_ROWS * c, PAIR_ROWS * min(c + CHUNK_PAIRS, last)) for c in range(first, last, CHUNK_PAIRS)
-            ]
+            odd = (last - first) % CHUNK_PAIRS
+            inner = range(first + odd, last, CHUNK_PAIRS) if h == 0 else range(first + 1, last)
+            edges = [first] + list(inner) + [last]
+            return [slice(PAIR_ROWS * a, PAIR_ROWS * b) for a, b in zip(edges, edges[1:]) if b > a]
 
         def logarithm(h):
             for cols in chunks(h):

@@ -59,7 +59,7 @@ def tile_mamba3mimoblock_pa_kernel(
 
     with ExitStack() as stack:
         keep = stack.enter_context(tc.tile_pool(name="keep", bufs=1))
-        stage = stack.enter_context(tc.tile_pool(name="stage", bufs=2))
+        stage = stack.enter_context(tc.tile_pool(name="stage", bufs=3))
         turned = stack.enter_context(tc.tile_pool(name="turned", bufs=3))
         banks = stack.enter_context(tc.psum_pool(name="banks", bufs=5))
         sums = stack.enter_context(tc.psum_pool(name="sums", bufs=3))
@@ -84,8 +84,9 @@ def tile_mamba3mimoblock_pa_kernel(
         decay = keep.tile([P, ROWS], F32)
 
         def load_x(i):
-            for h in range(2):
-                part = (slice(None), slice(PAIR * i, PAIR * (i + 1)), slice(K // 2 * h, K // 2 * (h + 1)))
+            cuts = (0, K_PASS, 2 * K_PASS, K) if i == 0 else (0, K // 2, K)
+            for a, b in zip(cuts, cuts[1:]):
+                part = (slice(None), slice(PAIR * i, PAIR * (i + 1)), slice(a, b))
                 nc.sync.dma_start(out=x_sb[part], in_=x_rows[part])
 
         def load_weight_codes(w, words):
@@ -94,13 +95,13 @@ def tile_mamba3mimoblock_pa_kernel(
                 in_=words.rearrange("g p n t -> p g (n t)").bitcast(I32),
             )
 
-        def load_weight_scales(queue, view, w, scales):
+        def load_weight_scales(w, scales):
             by_r = scales.rearrange("g (a r) n -> r a g n", r=4)
             for r in range(4):
-                queue.dma_start(out=w_scales[r:P:32, w].bitcast(view), in_=by_r[r].bitcast(view))
+                nc.sync.dma_start(out=w_scales[r:P:32, w].bitcast(I32), in_=by_r[r].bitcast(I32))
 
-        nc.vector.memset(w_scales[:].rearrange("p w g n -> p (w g n)").bitcast(I32), 0)
         masks.make_identity(nc, ident[:])
+        nc.vector.memset(w_scales[:].rearrange("p w g n -> p (w g n)").bitcast(I32), 0)
 
         vec_rows = keep.tile([P, P], BF16)
         nc.vector.memset(vec_rows[:], 0.0)
@@ -110,22 +111,22 @@ def tile_mamba3mimoblock_pa_kernel(
         nc.vector.memset(warm[:], 0.0)
         nc.scalar.mul(out=half_pi[:], in_=half_pi[:], mul=math.pi)
 
-        load_weight_scales(nc.scalar, F32, DT, W_dt_scales)
         load_x(0)
-        load_weight_scales(nc.scalar, F32, PH, W_ph_scales)
         load_x(1)
+        load_weight_scales(DT, W_dt_scales)
         load_weight_codes(DT, W_dt_words)
+        load_x(2)
+        load_weight_scales(PH, W_ph_scales)
         load_weight_codes(PH, W_ph_words)
         for j, vec in enumerate((b_dt, b_ph, A_real, A_imag)):
-            nc.sync.dma_start(out=vec_rows[j : j + 1, :], in_=vec.rearrange("(o n) -> o n", o=1))
-        load_x(2)
+            nc.gpsimd.dma_start(out=vec_rows[j : j + 1, :], in_=vec.rearrange("(o n) -> o n", o=1))
         load_x(3)
         nc.sync.dma_start(out=state[:, 1], in_=state_re.rearrange("(p t) c -> p t c", t=ROW_TILES))
         nc.sync.dma_start(out=state[:, 2], in_=state_im.rearrange("(p t) c -> p t c", t=ROW_TILES))
         for i in range(4, PAIRS):
             load_x(i)
         load_weight_codes(BV, W_B_words)
-        load_weight_scales(nc.sync, I32, BV, W_B_scales)
+        load_weight_scales(BV, W_B_scales)
 
         grouped_of = {}
 
@@ -179,10 +180,10 @@ def tile_mamba3mimoblock_pa_kernel(
         def first_functions(i):
             acc = acc_of[i]
             cols = slice(PAIR_ROWS * i, PAIR_ROWS * (i + 1))
-            nc.scalar.activation(out=soft[:, cols], in_=acc[:, DT, :], func=FUNC.Exp, bias=bias_dt[:])
+            nc.scalar.activation(out=soft[:, cols], in_=acc[:, DT, :], func=FUNC.Exp, bias=bias_dt)
             if i < FIRST_BATCH:
-                nc.scalar.activation(out=lin[:, cols], in_=acc[:, DT, :], func=FUNC.Identity, bias=bias_dt[:])
-            nc.scalar.activation(out=turn[:, cols], in_=acc[:, PH, :], func=FUNC.Tanh, bias=bias_ph[:])
+                nc.scalar.activation(out=lin[:, cols], in_=acc[:, DT, :], func=FUNC.Identity, bias=bias_dt)
+            nc.scalar.activation(out=turn[:, cols], in_=acc[:, PH, :], func=FUNC.Tanh, bias=bias_ph)
             capper = nc.gpsimd if i < FIRST_BATCH else nc.vector
             capper.tensor_scalar(
                 out=soft[:, cols], in0=soft[:, cols], scalar1=EXP_CAP, scalar2=1.0, op0=ALU.min, op1=ALU.add
@@ -198,19 +199,19 @@ def tile_mamba3mimoblock_pa_kernel(
 
         def spread_vectors():
             vec_f32 = keep.tile([P, P], F32)
-            nc.vector.tensor_copy(out=vec_f32[:], in_=vec_rows[:])
-            vec_cols = banks.tile([P, P], F32, tag="bank")
-            nc.tensor.transpose(out=vec_cols[:], in_=vec_f32[:], identity=ident[:])
-            nc.vector.tensor_copy(out=bias_dt[:], in_=vec_cols[:, 0:1])
-            nc.vector.tensor_copy(out=bias_ph[:], in_=vec_cols[:, 1:2])
-            nc.vector.tensor_copy(out=a_real[:], in_=vec_cols[:, 2:3])
-            nc.vector.tensor_scalar_mul(out=turns_per_dt[:], in0=vec_cols[:, 3:4], scalar1=1.0 / math.pi)
-            nc.scalar.activation(out=neg_rate[:], in_=a_real[:], func=FUNC.Exp)
-            nc.vector.tensor_scalar_mul(out=neg_rate[:], in0=neg_rate[:], scalar1=-1.0)
+            nc.gpsimd.tensor_copy(out=vec_f32[:], in_=vec_rows[:])
+            turned_rows = banks.tile([P, P], F32, tag="bank")
+            nc.tensor.transpose(out=turned_rows[:], in_=vec_f32[:], identity=ident[:])
+            nc.vector.tensor_copy(out=vec_cols[:], in_=turned_rows[:, 0:4])
+            nc.scalar.activation(out=neg_rate[:], in_=vec_cols[:, 2:3], func=FUNC.Exp)
+            nc.gpsimd.tensor_scalar(out=neg_rate[:], in0=neg_rate[:], scalar1=-1.0, scalar2=0.0, op0=ALU.mult, op1=ALU.add)
+            nc.gpsimd.tensor_scalar(
+                out=turns_per_dt[:], in0=vec_cols[:, 3:4], scalar1=1.0 / math.pi, scalar2=0.0, op0=ALU.mult, op1=ALU.add
+            )
 
-        bias_dt = keep.tile([P, 1], F32)
-        bias_ph = keep.tile([P, 1], F32)
-        a_real = keep.tile([P, 1], F32)
+        vec_cols = keep.tile([P, 4], F32)
+        bias_dt = vec_cols[:, 0:1]
+        bias_ph = vec_cols[:, 1:2]
         turns_per_dt = keep.tile([P, 1], F32)
         neg_rate = keep.tile([P, 1], F32)
 
@@ -233,7 +234,7 @@ def tile_mamba3mimoblock_pa_kernel(
                 for i in range(FIRST_BATCH, PAIRS):
                     cols = slice(PAIR_ROWS * i, PAIR_ROWS * (i + 1))
                     nc.vector.scalar_tensor_tensor(
-                        out=soft[:, cols], in0=acc_of[i][:, DT, :], scalar=bias_dt[:], in1=soft[:, cols],
+                        out=soft[:, cols], in0=acc_of[i][:, DT, :], scalar=bias_dt, in1=soft[:, cols],
                         op0=ALU.add, op1=ALU.max,
                     )
 
@@ -318,9 +319,12 @@ def tile_mamba3mimoblock_pa_kernel(
         transpose_x(0)
         quantise_x(0)
         transpose_x(1)
+        quantise_x(1)
+        transpose_x(2)
         spread_vectors()
         project(0)
-        for i in range(2, FIRST_BATCH + 1):
+        project(1)
+        for i in range(3, FIRST_BATCH + 1):
             stream(i)
             if i == FIRST_BATCH - 1:
                 nc.vector.tensor_scalar_mul(out=state[:, 0], in0=state[:, 2], scalar1=-1.0)

@@ -25,6 +25,7 @@ PAIR = 2
 PAIR_ROWS = PAIR * P
 PAIRS = ROW_TILES // PAIR
 FIRST_BATCH = 5
+BY_TANH = 6
 CHUNK_PAIRS = 2
 DT = 0
 PH = 1
@@ -101,25 +102,26 @@ def tile_mamba3mimoblock_pa_kernel(
                 nc.sync.dma_start(out=w_scales[r:P:32, w].bitcast(I32), in_=by_r[r].bitcast(I32))
 
         masks.make_identity(nc, ident[:])
-        nc.vector.memset(w_scales[:].rearrange("p w g n -> p (w g n)").bitcast(I32), 0)
-
         vec_rows = keep.tile([P, P], BF16)
         nc.vector.memset(vec_rows[:], 0.0)
+        nc.vector.memset(w_scales[:].rearrange("p w g n -> p (w g n)").bitcast(I32), 0)
+
+        half = keep.tile([P, 1], F32)
+        nc.vector.memset(half[:], 0.5)
         half_pi = keep.tile([P, 1], F32)
-        nc.vector.memset(half_pi[:], 0.5)
         warm = keep.tile([P, 1], F32)
         nc.vector.memset(warm[:], 0.0)
-        nc.scalar.mul(out=half_pi[:], in_=half_pi[:], mul=math.pi)
+        nc.scalar.mul(out=half_pi[:], in_=half[:], mul=math.pi)
 
         load_x(0)
+        for j, vec in enumerate((b_dt, b_ph, A_real, A_imag)):
+            nc.sync.dma_start(out=vec_rows[j : j + 1, :], in_=vec.rearrange("(o n) -> o n", o=1))
         load_x(1)
         load_weight_scales(DT, W_dt_scales)
         load_weight_codes(DT, W_dt_words)
         load_x(2)
         load_weight_scales(PH, W_ph_scales)
         load_weight_codes(PH, W_ph_words)
-        for j, vec in enumerate((b_dt, b_ph, A_real, A_imag)):
-            nc.gpsimd.dma_start(out=vec_rows[j : j + 1, :], in_=vec.rearrange("(o n) -> o n", o=1))
         load_x(3)
         nc.sync.dma_start(out=state[:, 1], in_=state_re.rearrange("(p t) c -> p t c", t=ROW_TILES))
         nc.sync.dma_start(out=state[:, 2], in_=state_im.rearrange("(p t) c -> p t c", t=ROW_TILES))
@@ -180,6 +182,11 @@ def tile_mamba3mimoblock_pa_kernel(
         def first_functions(i):
             acc = acc_of[i]
             cols = slice(PAIR_ROWS * i, PAIR_ROWS * (i + 1))
+            if i >= BY_TANH:
+                nc.scalar.activation(out=soft[:, cols], in_=acc[:, DT, :], func=FUNC.Abs, bias=bias_dt)
+                nc.scalar.activation(out=soft[:, cols], in_=soft[:, cols], func=FUNC.Tanh, scale=0.5)
+                nc.scalar.activation(out=turn[:, cols], in_=acc[:, PH, :], func=FUNC.Tanh, bias=bias_ph)
+                return
             nc.scalar.activation(out=soft[:, cols], in_=acc[:, DT, :], func=FUNC.Exp, bias=bias_dt)
             if i < FIRST_BATCH:
                 nc.scalar.activation(out=lin[:, cols], in_=acc[:, DT, :], func=FUNC.Identity, bias=bias_dt)
@@ -187,6 +194,12 @@ def tile_mamba3mimoblock_pa_kernel(
             capper = nc.gpsimd if i < FIRST_BATCH else nc.vector
             capper.tensor_scalar(
                 out=soft[:, cols], in0=soft[:, cols], scalar1=EXP_CAP, scalar2=1.0, op0=ALU.min, op1=ALU.add
+            )
+
+        def rectify(i):
+            cols = slice(PAIR_ROWS * i, PAIR_ROWS * (i + 1))
+            nc.vector.tensor_scalar(
+                out=lin[:, cols], in0=acc_of[i][:, DT, :], scalar1=bias_dt, scalar2=0.0, op0=ALU.add, op1=ALU.max
             )
 
         def stream(i):
@@ -199,15 +212,13 @@ def tile_mamba3mimoblock_pa_kernel(
 
         def spread_vectors():
             vec_f32 = keep.tile([P, P], F32)
-            nc.gpsimd.tensor_copy(out=vec_f32[:], in_=vec_rows[:])
+            nc.vector.tensor_copy(out=vec_f32[:], in_=vec_rows[:])
             turned_rows = banks.tile([P, P], F32, tag="bank")
             nc.tensor.transpose(out=turned_rows[:], in_=vec_f32[:], identity=ident[:])
             nc.vector.tensor_copy(out=vec_cols[:], in_=turned_rows[:, 0:4])
             nc.scalar.activation(out=neg_rate[:], in_=vec_cols[:, 2:3], func=FUNC.Exp)
-            nc.gpsimd.tensor_scalar(out=neg_rate[:], in0=neg_rate[:], scalar1=-1.0, scalar2=0.0, op0=ALU.mult, op1=ALU.add)
-            nc.gpsimd.tensor_scalar(
-                out=turns_per_dt[:], in0=vec_cols[:, 3:4], scalar1=1.0 / math.pi, scalar2=0.0, op0=ALU.mult, op1=ALU.add
-            )
+            nc.vector.tensor_scalar_mul(out=neg_rate[:], in0=neg_rate[:], scalar1=-1.0)
+            nc.vector.tensor_scalar_mul(out=turns_per_dt[:], in0=vec_cols[:, 3:4], scalar1=1.0 / math.pi)
 
         vec_cols = keep.tile([P, 4], F32)
         bias_dt = vec_cols[:, 0:1]
@@ -224,14 +235,20 @@ def tile_mamba3mimoblock_pa_kernel(
 
         def logarithm(h):
             for cols in chunks(h):
-                nc.scalar.activation(out=soft[:, cols], in_=soft[:, cols], func=FUNC.Ln)
+                if cols.start < PAIR_ROWS * BY_TANH:
+                    nc.scalar.activation(out=soft[:, cols], in_=soft[:, cols], func=FUNC.Ln)
+                else:
+                    nc.scalar.activation(out=soft[:, cols], in_=soft[:, cols], func=FUNC.Ln, scale=0.5, bias=half[:])
 
         def step_size(h):
             if h == 0:
                 for cols in chunks(h):
                     nc.vector.tensor_tensor(out=soft[:, cols], in0=soft[:, cols], in1=lin[:, cols], op=ALU.max)
             else:
-                for i in range(FIRST_BATCH, PAIRS):
+                for i in range(BY_TANH, PAIRS):
+                    cols = slice(PAIR_ROWS * i, PAIR_ROWS * (i + 1))
+                    nc.vector.tensor_tensor(out=soft[:, cols], in0=lin[:, cols], in1=soft[:, cols], op=ALU.subtract)
+                for i in range(FIRST_BATCH, BY_TANH):
                     cols = slice(PAIR_ROWS * i, PAIR_ROWS * (i + 1))
                     nc.vector.scalar_tensor_tensor(
                         out=soft[:, cols], in0=acc_of[i][:, DT, :], scalar=bias_dt, in1=soft[:, cols],
@@ -257,13 +274,8 @@ def tile_mamba3mimoblock_pa_kernel(
 
         def sin_and_cos(h):
             for cols in chunks(h):
-                if h == 0:
-                    nc.scalar.activation(out=cosd[:, cols], in_=frac[:, cols], func=FUNC.Abs)
-                else:
-                    nc.vector.scalar_tensor_tensor(
-                        out=cosd[:, cols], in0=frac[:, cols], scalar=-1.0, in1=frac[:, cols], op0=ALU.mult, op1=ALU.max
-                    )
                 nc.scalar.activation(out=sind[:, cols], in_=frac[:, cols], func=FUNC.Sin, scale=math.pi)
+                nc.scalar.activation(out=cosd[:, cols], in_=frac[:, cols], func=FUNC.Abs)
                 nc.scalar.activation(
                     out=cosd[:, cols], in_=cosd[:, cols], func=FUNC.Sin, scale=-math.pi, bias=half_pi[:]
                 )
@@ -319,9 +331,9 @@ def tile_mamba3mimoblock_pa_kernel(
         transpose_x(0)
         quantise_x(0)
         transpose_x(1)
+        spread_vectors()
         quantise_x(1)
         transpose_x(2)
-        spread_vectors()
         project(0)
         project(1)
         for i in range(3, FIRST_BATCH + 1):
@@ -329,28 +341,34 @@ def tile_mamba3mimoblock_pa_kernel(
             if i == FIRST_BATCH - 1:
                 nc.vector.tensor_scalar_mul(out=state[:, 0], in0=state[:, 2], scalar1=-1.0)
         logarithm(0)
-        quantise_x(FIRST_BATCH)
-        transpose_x(FIRST_BATCH + 1)
+        quantise_x(5)
+        transpose_x(6)
         step_size(0)
+        multiply(5)
+        quantise_x(6)
         decay_factor(0)
         angle(0)
-        multiply(FIRST_BATCH)
-        quantise_x(FIRST_BATCH + 1)
-        transpose_x(FIRST_BATCH + 2)
+        first_functions(5)
+        transpose_x(7)
+        nc.scalar.activation(out=warm[:], in_=warm[:], func=FUNC.Silu)
         b_products(0)
         sin_and_cos(0)
-        for cols in chunks(0):
-            scale_by_decay(cols, nc.gpsimd)
-        first_functions(FIRST_BATCH)
-        project(FIRST_BATCH + 1)
-        quantise_x(FIRST_BATCH + 2)
-        project(FIRST_BATCH + 2)
+        for n, cols in enumerate(chunks(0)):
+            scale_by_decay(cols, nc.vector if n == 0 else nc.gpsimd)
+        multiply(6)
+        rectify(6)
+        quantise_x(7)
+        rotate(0)
+        multiply(7)
+        rectify(7)
+        first_functions(6)
+        first_functions(7)
         logarithm(1)
         step_size(1)
         decay_factor(1)
         nc.scalar.activation(out=warm[:], in_=warm[:], func=FUNC.Sin)
         angle(1)
-        for i in range(FIRST_BATCH):
+        for i in range(1, FIRST_BATCH):
             rotate(i)
         b_products(1)
         sin_and_cos(1)

@@ -145,7 +145,7 @@ def tile_mamba3mimoblock_pa_kernel(
                             in_=words[:, WORDS * g + u : WORDS * (g + 1) : 2],
                             identity=ident[:],
                         )
-                copy = nc.scalar.copy if g % 2 == 0 else nc.vector.tensor_copy
+                copy = nc.scalar.copy if g in ((2,) if i in (5, 7) else (0, 2)) else nc.vector.tensor_copy
                 copy(
                     out=grouped[:, g, :].bitcast(F32).rearrange("p (r u) -> p r u", u=2),
                     in_=flipped[:].rearrange("p u r -> p r u"),
@@ -354,7 +354,8 @@ def tile_mamba3mimoblock_pa_kernel(
         b_products(0)
         sin_and_cos(0)
         for n, cols in enumerate(chunks(0)):
-            scale_by_decay(cols, nc.vector if n == 0 else nc.gpsimd)
+            (nc.vector if n <= 1 else nc.gpsimd).tensor_tensor(out=sind[:, cols], in0=sind[:, cols], in1=decay[:, cols], op=ALU.mult)
+            (nc.vector if n == 0 else nc.gpsimd).tensor_tensor(out=cosd[:, cols], in0=cosd[:, cols], in1=decay[:, cols], op=ALU.mult)
         multiply(6)
         rectify(6)
         quantise_x(7)
@@ -373,6 +374,7 @@ def tile_mamba3mimoblock_pa_kernel(
         b_products(1)
         sin_and_cos(1)
         for cols in chunks(1):
-            scale_by_decay(cols, nc.vector)
+            nc.gpsimd.tensor_tensor(out=sind[:, cols], in0=sind[:, cols], in1=decay[:, cols], op=ALU.mult)
+            nc.vector.tensor_tensor(out=cosd[:, cols], in0=cosd[:, cols], in1=decay[:, cols], op=ALU.mult)
         for i in range(FIRST_BATCH, PAIRS):
             rotate(i)

@@ -24,8 +24,7 @@ ROW_TILES = ROWS // P
 PAIR = 2
 PAIR_ROWS = PAIR * P
 PAIRS = ROW_TILES // PAIR
-FIRST_BATCH = 5
-BY_TANH = 6
+FIRST_BATCH = 4
 CHUNK_PAIRS = 2
 DT = 0
 PH = 1
@@ -62,8 +61,8 @@ def tile_mamba3mimoblock_pa_kernel(
         keep = stack.enter_context(tc.tile_pool(name="keep", bufs=1))
         stage = stack.enter_context(tc.tile_pool(name="stage", bufs=3))
         turned = stack.enter_context(tc.tile_pool(name="turned", bufs=3))
-        banks = stack.enter_context(tc.psum_pool(name="banks", bufs=5))
-        sums = stack.enter_context(tc.psum_pool(name="sums", bufs=3))
+        banks = stack.enter_context(tc.psum_pool(name="banks", bufs=6))
+        sums = stack.enter_context(tc.psum_pool(name="sums", bufs=2))
         stack.enter_context(
             tc.manual_schedule(engines={mybir.EngineType.PE, mybir.EngineType.Activation, mybir.EngineType.SP})
         )
@@ -182,25 +181,18 @@ def tile_mamba3mimoblock_pa_kernel(
         def first_functions(i):
             acc = acc_of[i]
             cols = slice(PAIR_ROWS * i, PAIR_ROWS * (i + 1))
-            if i >= BY_TANH:
+            if i < FIRST_BATCH:
+                nc.scalar.activation(out=soft[:, cols], in_=acc[:, DT, :], func=FUNC.Exp, bias=bias_dt)
+                nc.scalar.activation(out=lin[:, cols], in_=acc[:, DT, :], func=FUNC.Identity, bias=bias_dt)
+                nc.scalar.activation(out=turn[:, cols], in_=acc[:, PH, :], func=FUNC.Tanh, bias=bias_ph)
+                nc.gpsimd.tensor_scalar(
+                    out=soft[:, cols], in0=soft[:, cols], scalar1=EXP_CAP, scalar2=1.0, op0=ALU.min, op1=ALU.add
+                )
+            else:
                 nc.scalar.activation(out=soft[:, cols], in_=acc[:, DT, :], func=FUNC.Abs, bias=bias_dt)
                 nc.scalar.activation(out=soft[:, cols], in_=soft[:, cols], func=FUNC.Tanh, scale=0.5)
                 nc.scalar.activation(out=turn[:, cols], in_=acc[:, PH, :], func=FUNC.Tanh, bias=bias_ph)
-                return
-            nc.scalar.activation(out=soft[:, cols], in_=acc[:, DT, :], func=FUNC.Exp, bias=bias_dt)
-            if i < FIRST_BATCH:
-                nc.scalar.activation(out=lin[:, cols], in_=acc[:, DT, :], func=FUNC.Identity, bias=bias_dt)
-            nc.scalar.activation(out=turn[:, cols], in_=acc[:, PH, :], func=FUNC.Tanh, bias=bias_ph)
-            capper = nc.gpsimd if i < FIRST_BATCH else nc.vector
-            capper.tensor_scalar(
-                out=soft[:, cols], in0=soft[:, cols], scalar1=EXP_CAP, scalar2=1.0, op0=ALU.min, op1=ALU.add
-            )
-
-        def rectify(i):
-            cols = slice(PAIR_ROWS * i, PAIR_ROWS * (i + 1))
-            nc.vector.tensor_scalar(
-                out=lin[:, cols], in0=acc_of[i][:, DT, :], scalar1=bias_dt, scalar2=0.0, op0=ALU.add, op1=ALU.max
-            )
+                nc.scalar.activation(out=lin[:, cols], in_=acc[:, DT, :], func=FUNC.Relu, bias=bias_dt)
 
         def stream(i):
             if i >= 1:
@@ -227,33 +219,22 @@ def tile_mamba3mimoblock_pa_kernel(
         neg_rate = keep.tile([P, 1], F32)
 
         def chunks(h):
-            first, last = ((0, FIRST_BATCH), (FIRST_BATCH, PAIRS))[h]
-            odd = (last - first) % CHUNK_PAIRS
-            inner = range(first + odd, last, CHUNK_PAIRS) if h == 0 else range(first + 1, last)
-            edges = [first] + list(inner) + [last]
-            return [slice(PAIR_ROWS * a, PAIR_ROWS * b) for a, b in zip(edges, edges[1:]) if b > a]
+            edges = ((0, 1, 2, FIRST_BATCH), range(FIRST_BATCH, PAIRS + 1))[h]
+            return [slice(PAIR_ROWS * a, PAIR_ROWS * b) for a, b in zip(edges, edges[1:])]
 
         def logarithm(h):
             for cols in chunks(h):
-                if cols.start < PAIR_ROWS * BY_TANH:
+                if h == 0:
                     nc.scalar.activation(out=soft[:, cols], in_=soft[:, cols], func=FUNC.Ln)
                 else:
                     nc.scalar.activation(out=soft[:, cols], in_=soft[:, cols], func=FUNC.Ln, scale=0.5, bias=half[:])
 
         def step_size(h):
-            if h == 0:
-                for cols in chunks(h):
+            for cols in chunks(h):
+                if h == 0:
                     nc.vector.tensor_tensor(out=soft[:, cols], in0=soft[:, cols], in1=lin[:, cols], op=ALU.max)
-            else:
-                for i in range(BY_TANH, PAIRS):
-                    cols = slice(PAIR_ROWS * i, PAIR_ROWS * (i + 1))
+                else:
                     nc.vector.tensor_tensor(out=soft[:, cols], in0=lin[:, cols], in1=soft[:, cols], op=ALU.subtract)
-                for i in range(FIRST_BATCH, BY_TANH):
-                    cols = slice(PAIR_ROWS * i, PAIR_ROWS * (i + 1))
-                    nc.vector.scalar_tensor_tensor(
-                        out=soft[:, cols], in0=acc_of[i][:, DT, :], scalar=bias_dt, in1=soft[:, cols],
-                        op0=ALU.add, op1=ALU.max,
-                    )
 
         def decay_factor(h):
             for cols in chunks(h):
@@ -271,18 +252,24 @@ def tile_mamba3mimoblock_pa_kernel(
                 nc.vector.scalar_tensor_tensor(
                     out=frac[:, cols], in0=whole[:, cols], scalar=-2.0, in1=turn[:, cols], op0=ALU.mult, op1=ALU.add
                 )
+            if h == 1:
+                for cols in chunks(h):
+                    nc.vector.scalar_tensor_tensor(
+                        out=cosd[:, cols], in0=frac[:, cols], scalar=-1.0, in1=frac[:, cols], op0=ALU.mult, op1=ALU.max
+                    )
 
         def sin_and_cos(h):
             for cols in chunks(h):
                 nc.scalar.activation(out=sind[:, cols], in_=frac[:, cols], func=FUNC.Sin, scale=math.pi)
-                nc.scalar.activation(out=cosd[:, cols], in_=frac[:, cols], func=FUNC.Abs)
+                if h == 0:
+                    nc.scalar.activation(out=cosd[:, cols], in_=frac[:, cols], func=FUNC.Abs)
                 nc.scalar.activation(
                     out=cosd[:, cols], in_=cosd[:, cols], func=FUNC.Sin, scale=-math.pi, bias=half_pi[:]
                 )
 
-        def scale_by_decay(cols, engine):
-            engine.tensor_tensor(out=sind[:, cols], in0=sind[:, cols], in1=decay[:, cols], op=ALU.mult)
-            engine.tensor_tensor(out=cosd[:, cols], in0=cosd[:, cols], in1=decay[:, cols], op=ALU.mult)
+        def scale_by_decay(cols, sine_engine, cosine_engine):
+            sine_engine.tensor_tensor(out=sind[:, cols], in0=sind[:, cols], in1=decay[:, cols], op=ALU.mult)
+            cosine_engine.tensor_tensor(out=cosd[:, cols], in0=cosd[:, cols], in1=decay[:, cols], op=ALU.mult)
 
         b_val_of = {}
 
@@ -338,31 +325,33 @@ def tile_mamba3mimoblock_pa_kernel(
         project(1)
         for i in range(3, FIRST_BATCH + 1):
             stream(i)
-            if i == FIRST_BATCH - 1:
-                nc.vector.tensor_scalar_mul(out=state[:, 0], in0=state[:, 2], scalar1=-1.0)
+        nc.vector.tensor_scalar_mul(out=state[:, 0], in0=state[:, 2], scalar1=-1.0)
         logarithm(0)
+        quantise_x(4)
+        transpose_x(5)
+        step_size(0)
         quantise_x(5)
         transpose_x(6)
-        step_size(0)
-        multiply(5)
-        quantise_x(6)
+        multiply(4)
         decay_factor(0)
         angle(0)
-        first_functions(5)
         transpose_x(7)
-        nc.scalar.activation(out=warm[:], in_=warm[:], func=FUNC.Silu)
+        multiply(5)
         b_products(0)
-        sin_and_cos(0)
-        for n, cols in enumerate(chunks(0)):
-            (nc.vector if n <= 1 else nc.gpsimd).tensor_tensor(out=sind[:, cols], in0=sind[:, cols], in1=decay[:, cols], op=ALU.mult)
-            (nc.vector if n == 0 else nc.gpsimd).tensor_tensor(out=cosd[:, cols], in0=cosd[:, cols], in1=decay[:, cols], op=ALU.mult)
+        first_functions(4)
+        first_functions(5)
+        quantise_x(6)
         multiply(6)
-        rectify(6)
+        nc.scalar.activation(out=warm[:], in_=warm[:], func=FUNC.Silu)
+        sin_and_cos(0)
         quantise_x(7)
+        first = chunks(0)
+        scale_by_decay(first[0], nc.gpsimd, nc.gpsimd)
+        scale_by_decay(first[1], nc.vector, nc.vector)
+        scale_by_decay(first[2], nc.vector, nc.gpsimd)
         rotate(0)
-        multiply(7)
-        rectify(7)
         first_functions(6)
+        multiply(7)
         first_functions(7)
         logarithm(1)
         step_size(1)
@@ -373,8 +362,8 @@ def tile_mamba3mimoblock_pa_kernel(
             rotate(i)
         b_products(1)
         sin_and_cos(1)
-        for cols in chunks(1):
-            nc.gpsimd.tensor_tensor(out=sind[:, cols], in0=sind[:, cols], in1=decay[:, cols], op=ALU.mult)
-            nc.vector.tensor_tensor(out=cosd[:, cols], in0=cosd[:, cols], in1=decay[:, cols], op=ALU.mult)
+        last = chunks(1)
+        for cols in last:
+            scale_by_decay(cols, nc.gpsimd, nc.vector)
         for i in range(FIRST_BATCH, PAIRS):
             rotate(i)

@@ -25,6 +25,8 @@ PAIR = 2
 PAIR_ROWS = PAIR * P
 PAIRS = ROW_TILES // PAIR
 FIRST_BATCH = 4
+SPLIT_PAIRS = (1, 2, 3)
+SPLIT_GROUP = 3
 CHUNK_PAIRS = 2
 DT = 0
 PH = 1
@@ -59,7 +61,8 @@ def tile_mamba3mimoblock_pa_kernel(
 
     with ExitStack() as stack:
         keep = stack.enter_context(tc.tile_pool(name="keep", bufs=1))
-        stage = stack.enter_context(tc.tile_pool(name="stage", bufs=3))
+        stage = stack.enter_context(tc.tile_pool(name="stage", bufs=2))
+        splits = stack.enter_context(tc.tile_pool(name="splits", bufs=2))
         turned = stack.enter_context(tc.tile_pool(name="turned", bufs=3))
         banks = stack.enter_context(tc.psum_pool(name="banks", bufs=6))
         sums = stack.enter_context(tc.psum_pool(name="sums", bufs=2))
@@ -130,6 +133,13 @@ def tile_mamba3mimoblock_pa_kernel(
         load_weight_scales(BV, W_B_scales)
 
         grouped_of = {}
+        split_of = {}
+
+        def split_words(i):
+            if i in SPLIT_PAIRS:
+                split_of[i] = splits.tile([P, PAIR, 2, P], F32, name="split")
+                row_words = x_sb[:, PAIR * i : PAIR * (i + 1), K_PASS * SPLIT_GROUP : K_PASS * (SPLIT_GROUP + 1)].bitcast(F32)
+                nc.scalar.copy(out=split_of[i][:], in_=row_words.rearrange("p j (q u) -> p j u q", u=2))
 
         def transpose_x(i):
             grouped = stage.tile([P, GROUPS, 4 * PAIR_ROWS], BF16, align_bytes=64)
@@ -141,7 +151,11 @@ def tile_mamba3mimoblock_pa_kernel(
                     for u in range(2):
                         nc.tensor.transpose(
                             out=flipped[:, u, P * j : P * (j + 1)],
-                            in_=words[:, WORDS * g + u : WORDS * (g + 1) : 2],
+                            in_=(
+                                split_of[i][:, j, u, :]
+                                if i in split_of and g == SPLIT_GROUP
+                                else words[:, WORDS * g + u : WORDS * (g + 1) : 2]
+                            ),
                             identity=ident[:],
                         )
                 copy = nc.scalar.copy if g in ((2,) if i in (5, 7) else (0, 2)) else nc.vector.tensor_copy
@@ -199,6 +213,7 @@ def tile_mamba3mimoblock_pa_kernel(
                 quantise_x(i - 1)
             if i < PAIRS:
                 transpose_x(i)
+            split_words(i + 1)
             if i >= 1:
                 project(i - 1)
 
@@ -310,17 +325,24 @@ def tile_mamba3mimoblock_pa_kernel(
                 out=by_sin[:], in0=state[:, 0:2, tiles, :], in1=cos_sin[:, 1:2].to_broadcast(both), op=ALU.mult
             )
             nc.vector.tensor_tensor(out=by_cos[:, 0], in0=by_cos[:, 0], in1=b_val_of[i], op=ALU.add)
-            adder = nc.vector if i == PAIRS - 1 else nc.gpsimd
-            adder.tensor_tensor(out=result[:], in0=by_cos[:], in1=by_sin[:], op=ALU.add)
-            for s in range(2):
-                nc.sync.dma_start(out=out_rows[s][:, tiles, :], in_=result[:, s])
+            if i < PAIRS - 1:
+                nc.gpsimd.tensor_tensor(out=result[:], in0=by_cos[:], in1=by_sin[:], op=ALU.add)
+                for s in range(2):
+                    nc.sync.dma_start(out=out_rows[s][:, tiles, :], in_=result[:, s])
+            else:
+                for s in (1, 0):
+                    nc.vector.tensor_tensor(out=result[:, s], in0=by_cos[:, s], in1=by_sin[:, s], op=ALU.add)
+                    nc.sync.dma_start(out=out_rows[s][:, tiles, :], in_=result[:, s])
 
         transpose_x(0)
+        split_words(1)
         quantise_x(0)
         transpose_x(1)
+        split_words(2)
         spread_vectors()
         quantise_x(1)
         transpose_x(2)
+        split_words(3)
         project(0)
         project(1)
         for i in range(3, FIRST_BATCH + 1):
@@ -345,10 +367,8 @@ def tile_mamba3mimoblock_pa_kernel(
         nc.scalar.activation(out=warm[:], in_=warm[:], func=FUNC.Silu)
         sin_and_cos(0)
         quantise_x(7)
-        first = chunks(0)
-        scale_by_decay(first[0], nc.gpsimd, nc.gpsimd)
-        scale_by_decay(first[1], nc.vector, nc.vector)
-        scale_by_decay(first[2], nc.vector, nc.gpsimd)
+        for cols in chunks(0):
+            scale_by_decay(cols, nc.vector, nc.gpsimd)
         rotate(0)
         first_functions(6)
         multiply(7)

@@ -87,7 +87,7 @@ def tile_mamba3mimoblock_pa_kernel(
         decay = keep.tile([P, ROWS], F32)
 
         def load_x(i):
-            cuts = (0, K_PASS, 2 * K_PASS, K) if i == 0 else (0, K // 2, K)
+            cuts = (0, K_PASS, 2 * K_PASS, K) if i == 0 else (0, K // 2, K) if i <= 2 else (0, K)
             for a, b in zip(cuts, cuts[1:]):
                 part = (slice(None), slice(PAIR * i, PAIR * (i + 1)), slice(a, b))
                 nc.sync.dma_start(out=x_sb[part], in_=x_rows[part])

@@ -124,11 +124,10 @@ def tile_mamba3mimoblock_pa_kernel(
         load_x(2)
         load_weight_scales(PH, W_ph_scales)
         load_weight_codes(PH, W_ph_words)
-        load_x(3)
+        for i in range(3, PAIRS):
+            load_x(i)
         nc.sync.dma_start(out=state[:, 1], in_=state_re.rearrange("(p t) c -> p t c", t=ROW_TILES))
         nc.sync.dma_start(out=state[:, 2], in_=state_im.rearrange("(p t) c -> p t c", t=ROW_TILES))
-        for i in range(4, PAIRS):
-            load_x(i)
         load_weight_codes(BV, W_B_words)
         load_weight_scales(BV, W_B_scales)
 
@@ -268,15 +267,15 @@ def tile_mamba3mimoblock_pa_kernel(
                     out=frac[:, cols], in0=whole[:, cols], scalar=-2.0, in1=turn[:, cols], op0=ALU.mult, op1=ALU.add
                 )
             if h == 1:
-                for cols in chunks(h):
+                for cols in chunks(h)[:-1]:
                     nc.vector.scalar_tensor_tensor(
                         out=cosd[:, cols], in0=frac[:, cols], scalar=-1.0, in1=frac[:, cols], op0=ALU.mult, op1=ALU.max
                     )
 
         def sin_and_cos(h):
-            for cols in chunks(h):
+            for n, cols in enumerate(chunks(h)):
                 nc.scalar.activation(out=sind[:, cols], in_=frac[:, cols], func=FUNC.Sin, scale=math.pi)
-                if h == 0:
+                if h == 0 or n == len(chunks(h)) - 1:
                     nc.scalar.activation(out=cosd[:, cols], in_=frac[:, cols], func=FUNC.Abs)
                 nc.scalar.activation(
                     out=cosd[:, cols], in_=cosd[:, cols], func=FUNC.Sin, scale=-math.pi, bias=half_pi[:]
@@ -347,7 +346,6 @@ def tile_mamba3mimoblock_pa_kernel(
         project(1)
         for i in range(3, FIRST_BATCH + 1):
             stream(i)
-        nc.vector.tensor_scalar_mul(out=state[:, 0], in0=state[:, 2], scalar1=-1.0)
         logarithm(0)
         quantise_x(4)
         transpose_x(5)
@@ -369,6 +367,7 @@ def tile_mamba3mimoblock_pa_kernel(
         quantise_x(7)
         for cols in chunks(0):
             scale_by_decay(cols, nc.vector, nc.gpsimd)
+        nc.vector.tensor_scalar_mul(out=state[:, 0], in0=state[:, 2], scalar1=-1.0)
         rotate(0)
         first_functions(6)
         multiply(7)

import math
from contextlib import ExitStack

import concourse.masks as masks
import concourse.mybir as mybir

F32 = mybir.dt.float32
BF16 = mybir.dt.bfloat16
I32 = mybir.dt.int32
U32 = mybir.dt.uint32
U8 = mybir.dt.uint8
FP8X4 = mybir.dt.float8_e4m3fn_x4
ALU = mybir.AluOpType
FUNC = mybir.ActivationFunctionType

P = 128
ROWS = 2048
K = 2048
CH = 128
K_PASS = 512
GROUPS = K // K_PASS
WORDS = K_PASS // 2
ROW_TILES = ROWS // P
PAIR = 2
PAIR_ROWS = PAIR * P
PAIRS = ROW_TILES // PAIR
FIRST_BATCH = 4
SPLIT_PAIRS = (1, 2, 3)
SPLIT_GROUP = 3
CHUNK_PAIRS = 2
DT = 0
PH = 1
BV = 2

EXP_CAP = math.exp(30.0)

FLOPS = 2 * ROWS * K * 3 * CH


def tile_mamba3mimoblock_pa_kernel(
    tc,
    x,
    state_re,
    state_im,
    W_dt_words,
    W_dt_scales,
    b_dt,
    W_ph_words,
    W_ph_scales,
    b_ph,
    W_B_words,
    W_B_scales,
    A_real,
    A_imag,
    out_0,
    out_1,
):
    nc = tc.nc
    x_rows = x.rearrange("(p t) k -> p t k", t=ROW_TILES)
    out_rows = [o.rearrange("(p t) c -> p t c", t=ROW_TILES) for o in (out_0, out_1)]

    with ExitStack() as stack:
        keep = stack.enter_context(tc.tile_pool(name="keep", bufs=1))
        stage = stack.enter_context(tc.tile_pool(name="stage", bufs=2))
        splits = stack.enter_context(tc.tile_pool(name="splits", bufs=2))
        turned = stack.enter_context(tc.tile_pool(name="turned", bufs=3))
        banks = stack.enter_context(tc.psum_pool(name="banks", bufs=6))
        sums = stack.enter_context(tc.psum_pool(name="sums", bufs=2))
        stack.enter_context(
            tc.manual_schedule(engines={mybir.EngineType.PE, mybir.EngineType.Activation, mybir.EngineType.SP})
        )

        x_sb = keep.tile([P, ROW_TILES, K], BF16)
        codes = keep.tile([P, PAIRS, GROUPS, PAIR_ROWS], U32, align_bytes=64)
        x_scales = keep.tile([P, PAIRS, GROUPS, PAIR_ROWS], U8, align_bytes=64)
        w_codes = keep.tile([P, 3, GROUPS, CH], U32, align_bytes=64)
        w_scales = keep.tile([P, 3, GROUPS, CH], U8, align_bytes=64)
        state = keep.tile([P, 3, ROW_TILES, CH], BF16)
        ident = keep.tile([P, P], F32)
        soft = keep.tile([P, ROWS], F32)
        lin = keep.tile([P, ROWS], F32)
        turn = keep.tile([P, ROWS], F32)
        whole = keep.tile([P, ROWS], I32)
        frac = keep.tile([P, ROWS], F32)
        cosd = keep.tile([P, ROWS], F32)
        sind = keep.tile([P, ROWS], F32)
        decay = keep.tile([P, ROWS], F32)

        def load_x(i):
            cuts = (0, K_PASS, 2 * K_PASS, K) if i == 0 else (0, K // 2, K) if i <= 2 else (0, K)
            for a, b in zip(cuts, cuts[1:]):
                part = (slice(None), slice(PAIR * i, PAIR * (i + 1)), slice(a, b))
                nc.sync.dma_start(out=x_sb[part], in_=x_rows[part])

        def load_weight_codes(w, words):
            nc.sync.dma_start(
                out=w_codes[:, w].bitcast(I32),
                in_=words.rearrange("g p n t -> p g (n t)").bitcast(I32),
            )

        def load_weight_scales(w, scales):
            by_r = scales.rearrange("g (a r) n -> r a g n", r=4)
            for r in range(4):
                nc.sync.dma_start(out=w_scales[r:P:32, w].bitcast(I32), in_=by_r[r].bitcast(I32))

        masks.make_identity(nc, ident[:])
        vec_rows = keep.tile([P, P], BF16)
        nc.vector.memset(vec_rows[:], 0.0)
        nc.vector.memset(w_scales[:].rearrange("p w g n -> p (w g n)").bitcast(I32), 0)

        half = keep.tile([P, 1], F32)
        nc.vector.memset(half[:], 0.5)
        half_pi = keep.tile([P, 1], F32)
        warm = keep.tile([P, 1], F32)
        nc.vector.memset(warm[:], 0.0)
        nc.scalar.mul(out=half_pi[:], in_=half[:], mul=math.pi)

        load_x(0)
        for j, vec in enumerate((b_dt, b_ph, A_real, A_imag)):
            nc.sync.dma_start(out=vec_rows[j : j + 1, :], in_=vec.rearrange("(o n) -> o n", o=1))
        load_x(1)
        load_weight_scales(DT, W_dt_scales)
        load_weight_codes(DT, W_dt_words)
        load_x(2)
        load_weight_scales(PH, W_ph_scales)
        load_weight_codes(PH, W_ph_words)
        for i in range(3, PAIRS):
            load_x(i)
        nc.sync.dma_start(out=state[:, 1], in_=state_re.rearrange("(p t) c -> p t c", t=ROW_TILES))
        nc.sync.dma_start(out=state[:, 2], in_=state_im.rearrange("(p t) c -> p t c", t=ROW_TILES))
        load_weight_codes(BV, W_B_words)
        load_weight_scales(BV, W_B_scales)

        grouped_of = {}
        split_of = {}

        def split_words(i):
            if i in SPLIT_PAIRS:
                split_of[i] = splits.tile([P, PAIR, 2, P], F32, name="split")
                row_words = x_sb[:, PAIR * i : PAIR * (i + 1), K_PASS * SPLIT_GROUP : K_PASS * (SPLIT_GROUP + 1)].bitcast(F32)
                nc.scalar.copy(out=split_of[i][:], in_=row_words.rearrange("p j (q u) -> p j u q", u=2))

        def transpose_x(i):
            grouped = stage.tile([P, GROUPS, 4 * PAIR_ROWS], BF16, align_bytes=64)
            grouped_of[i] = grouped
            for g in range(GROUPS):
                flipped = banks.tile([P, 2, PAIR_ROWS], F32, tag="bank")
                for j in range(PAIR):
                    words = x_sb[:, PAIR * i + j, :].bitcast(F32)
                    for u in range(2):
                        nc.tensor.transpose(
                            out=flipped[:, u, P * j : P * (j + 1)],
                            in_=(
                                split_of[i][:, j, u, :]
                                if i in split_of and g == SPLIT_GROUP
                                else words[:, WORDS * g + u : WORDS * (g + 1) : 2]
                            ),
                            identity=ident[:],
                        )
                copy = nc.scalar.copy if g in ((2,) if i in (5, 7) else (0, 2)) else nc.vector.tensor_copy
                copy(
                    out=grouped[:, g, :].bitcast(F32).rearrange("p (r u) -> p r u", u=2),
                    in_=flipped[:].rearrange("p u r -> p r u"),
                )

        def quantise_x(i):
            nc.vector.quantize_mx(
                out=codes[:, i].rearrange("p g r -> p (g r)").bitcast(FP8X4),
                scales=x_scales[:, i].rearrange("p g r -> p (g r)"),
                in_=grouped_of[i][:].rearrange("p g c -> p (g c)"),
            )

        def project(i):
            multiply(i)
            first_functions(i)

        acc_of = {}

        def multiply(i):
            acc = sums.tile([P, 2, PAIR_ROWS], F32)
            acc_of[i] = acc
            for w in (DT, PH):
                for g in range(GROUPS):
                    nc.tensor.matmul_mx(
                        out=acc[:, w, :],
                        lhsT=w_codes[:, w, g, :].bitcast(FP8X4),
                        lhsT_scale=w_scales[:, w, g, :],
                        rhs=codes[:, i, g, :].bitcast(FP8X4),
                        rhs_scale=x_scales[:, i, g, :],
                        start=(g == 0),
                        stop=(g == GROUPS - 1),
                    )

        def first_functions(i):
            acc = acc_of[i]
            cols = slice(PAIR_ROWS * i, PAIR_ROWS * (i + 1))
            if i < FIRST_BATCH:
                nc.scalar.activation(out=soft[:, cols], in_=acc[:, DT, :], func=FUNC.Exp, bias=bias_dt)
                nc.scalar.activation(out=lin[:, cols], in_=acc[:, DT, :], func=FUNC.Identity, bias=bias_dt)
                nc.scalar.activation(out=turn[:, cols], in_=acc[:, PH, :], func=FUNC.Tanh, bias=bias_ph)
                nc.gpsimd.tensor_scalar(
                    out=soft[:, cols], in0=soft[:, cols], scalar1=EXP_CAP, scalar2=1.0, op0=ALU.min, op1=ALU.add
                )
            else:
                nc.scalar.activation(out=soft[:, cols], in_=acc[:, DT, :], func=FUNC.Abs, bias=bias_dt)
                nc.scalar.activation(out=soft[:, cols], in_=soft[:, cols], func=FUNC.Tanh, scale=0.5)
                nc.scalar.activation(out=turn[:, cols], in_=acc[:, PH, :], func=FUNC.Tanh, bias=bias_ph)
                nc.scalar.activation(out=lin[:, cols], in_=acc[:, DT, :], func=FUNC.Relu, bias=bias_dt)

        def stream(i):
            if i >= 1:
                quantise_x(i - 1)
            if i < PAIRS:
                transpose_x(i)
            split_words(i + 1)
            if i >= 1:
                project(i - 1)

        def spread_vectors():
            vec_f32 = keep.tile([P, P], F32)
            nc.vector.tensor_copy(out=vec_f32[:], in_=vec_rows[:])
            turned_rows = banks.tile([P, P], F32, tag="bank")
            nc.tensor.transpose(out=turned_rows[:], in_=vec_f32[:], identity=ident[:])
            nc.vector.tensor_copy(out=vec_cols[:], in_=turned_rows[:, 0:4])
            nc.scalar.activation(out=neg_rate[:], in_=vec_cols[:, 2:3], func=FUNC.Exp)
            nc.vector.tensor_scalar_mul(out=neg_rate[:], in0=neg_rate[:], scalar1=-1.0)
            nc.vector.tensor_scalar_mul(out=turns_per_dt[:], in0=vec_cols[:, 3:4], scalar1=1.0 / math.pi)

        vec_cols = keep.tile([P, 4], F32)
        bias_dt = vec_cols[:, 0:1]
        bias_ph = vec_cols[:, 1:2]
        turns_per_dt = keep.tile([P, 1], F32)
        neg_rate = keep.tile([P, 1], F32)

        def chunks(h):
            edges = ((0, 1, 2, FIRST_BATCH), range(FIRST_BATCH, PAIRS + 1))[h]
            return [slice(PAIR_ROWS * a, PAIR_ROWS * b) for a, b in zip(edges, edges[1:])]

        def logarithm(h):
            for cols in chunks(h):
                if h == 0:
                    nc.scalar.activation(out=soft[:, cols], in_=soft[:, cols], func=FUNC.Ln)
                else:
                    nc.scalar.activation(out=soft[:, cols], in_=soft[:, cols], func=FUNC.Ln, scale=0.5, bias=half[:])

        def step_size(h):
            for cols in chunks(h):
                if h == 0:
                    nc.vector.tensor_tensor(out=soft[:, cols], in0=soft[:, cols], in1=lin[:, cols], op=ALU.max)
                else:
                    nc.vector.tensor_tensor(out=soft[:, cols], in0=lin[:, cols], in1=soft[:, cols], op=ALU.subtract)

        def decay_factor(h):
            for cols in chunks(h):
                nc.scalar.activation(out=decay[:, cols], in_=soft[:, cols], func=FUNC.Exp, scale=neg_rate[:])

        def angle(h):
            for cols in chunks(h):
                nc.vector.scalar_tensor_tensor(
                    out=turn[:, cols], in0=soft[:, cols], scalar=turns_per_dt[:], in1=turn[:, cols],
                    op0=ALU.mult, op1=ALU.add,
                )
            for cols in chunks(h):
                nc.vector.tensor_scalar_mul(out=whole[:, cols], in0=turn[:, cols], scalar1=0.5)
            for cols in chunks(h):
                nc.vector.scalar_tensor_tensor(
                    out=frac[:, cols], in0=whole[:, cols], scalar=-2.0, in1=turn[:, cols], op0=ALU.mult, op1=ALU.add
                )
            if h == 1:
                for cols in chunks(h)[:-1]:
                    nc.vector.scalar_tensor_tensor(
                        out=cosd[:, cols], in0=frac[:, cols], scalar=-1.0, in1=frac[:, cols], op0=ALU.mult, op1=ALU.max
                    )

        def sin_and_cos(h):
            for n, cols in enumerate(chunks(h)):
                nc.scalar.activation(out=sind[:, cols], in_=frac[:, cols], func=FUNC.Sin, scale=math.pi)
                if h == 0 or n == len(chunks(h)) - 1:
                    nc.scalar.activation(out=cosd[:, cols], in_=frac[:, cols], func=FUNC.Abs)
                nc.scalar.activation(
                    out=cosd[:, cols], in_=cosd[:, cols], func=FUNC.Sin, scale=-math.pi, bias=half_pi[:]
                )

        def scale_by_decay(cols, sine_engine, cosine_engine):
            sine_engine.tensor_tensor(out=sind[:, cols], in0=sind[:, cols], in1=decay[:, cols], op=ALU.mult)
            cosine_engine.tensor_tensor(out=cosd[:, cols], in0=cosd[:, cols], in1=decay[:, cols], op=ALU.mult)

        b_val_of = {}

        def b_products(h):
            first, last = ((0, FIRST_BATCH), (FIRST_BATCH, PAIRS))[h]
            for c in range(first, last, CHUNK_PAIRS):
                b_bank = banks.tile([P, CHUNK_PAIRS, PAIR, CH], F32, tag="bank")
                for i in range(c, min(c + CHUNK_PAIRS, last)):
                    b_val_of[i] = b_bank[:, i - c]
                    for j in range(PAIR):
                        rows = slice(P * j, P * (j + 1))
                        for g in range(GROUPS):
                            nc.tensor.matmul_mx(
                                out=b_bank[:, i - c, j, :],
                                lhsT=codes[:, i, g, rows].bitcast(FP8X4),
                                lhsT_scale=x_scales[:, i, g, rows],
                                rhs=w_codes[:, BV, g, :].bitcast(FP8X4),
                                rhs_scale=w_scales[:, BV, g, :],
                                start=(g == 0),
                                stop=(g == GROUPS - 1),
                            )

        def rotate(i):
            tiles = slice(PAIR * i, PAIR * (i + 1))
            cos_sin = banks.tile([P, 2, PAIR, CH], F32, tag="bank")
            for s, source in enumerate((cosd, sind)):
                for j in range(PAIR):
                    first = PAIR_ROWS * i + P * j
                    nc.tensor.transpose(out=cos_sin[:, s, j, :], in_=source[:, first : first + P], identity=ident[:])
            both = [P, 2, PAIR, CH]
            by_cos = turned.tile(both, F32)
            by_sin = turned.tile(both, F32)
            result = turned.tile(both, F32)
            nc.vector.tensor_tensor(
                out=by_cos[:], in0=state[:, 1:3, tiles, :], in1=cos_sin[:, 0:1].to_broadcast(both), op=ALU.mult
            )
            nc.vector.tensor_tensor(
                out=by_sin[:], in0=state[:, 0:2, tiles, :], in1=cos_sin[:, 1:2].to_broadcast(both), op=ALU.mult
            )
            nc.vector.tensor_tensor(out=by_cos[:, 0], in0=by_cos[:, 0], in1=b_val_of[i], op=ALU.add)
            if i < PAIRS - 1:
                nc.gpsimd.tensor_tensor(out=result[:], in0=by_cos[:], in1=by_sin[:], op=ALU.add)
                for s in range(2):
                    nc.sync.dma_start(out=out_rows[s][:, tiles, :], in_=result[:, s])
            else:
                for s in (1, 0):
                    nc.vector.tensor_tensor(out=result[:, s], in0=by_cos[:, s], in1=by_sin[:, s], op=ALU.add)
                    nc.sync.dma_start(out=out_rows[s][:, tiles, :], in_=result[:, s])

        transpose_x(0)
        split_words(1)
        quantise_x(0)
        transpose_x(1)
        split_words(2)
        spread_vectors()
        quantise_x(1)
        transpose_x(2)
        split_words(3)
        project(0)
        project(1)
        for i in range(3, FIRST_BATCH + 1):
            stream(i)
        logarithm(0)
        quantise_x(4)
        transpose_x(5)
        step_size(0)
        quantise_x(5)
        transpose_x(6)
        multiply(4)
        decay_factor(0)
        angle(0)
        transpose_x(7)
        multiply(5)
        b_products(0)
        first_functions(4)
        first_functions(5)
        quantise_x(6)
        multiply(6)
        nc.scalar.activation(out=warm[:], in_=warm[:], func=FUNC.Silu)
        sin_and_cos(0)
        quantise_x(7)
        for cols in chunks(0):
            scale_by_decay(cols, nc.vector, nc.gpsimd)
        nc.vector.tensor_scalar_mul(out=state[:, 0], in0=state[:, 2], scalar1=-1.0)
        rotate(0)
        first_functions(6)
        multiply(7)
        first_functions(7)
        logarithm(1)
        step_size(1)
        decay_factor(1)
        nc.scalar.activation(out=warm[:], in_=warm[:], func=FUNC.Sin)
        angle(1)
        for i in range(1, FIRST_BATCH):
            rotate(i)
        b_products(1)
        sin_and_cos(1)
        last = chunks(1)
        for cols in last:
            scale_by_decay(cols, nc.gpsimd, nc.vector)
        for i in range(FIRST_BATCH, PAIRS):
            rotate(i)
